import numpy as np
import ml_dtypes


def mxq(x, axis, fmt="e4m3"):
    dtype, down = {"e4m3": (ml_dtypes.float8_e4m3fn, 7), "e5m2": (ml_dtypes.float8_e5m2, 14)}[fmt]
    v = np.moveaxis(np.asarray(x, np.float32).astype(ml_dtypes.bfloat16).astype(np.float64), axis, -1)
    blocks = v.reshape(v.shape[:-1] + (-1, 32))
    amax = np.abs(blocks).max(-1, keepdims=True)
    byte = np.maximum(np.where(amax > 0, np.frexp(amax)[1] - 1 + 127, 0) - down, 1)
    scale = np.exp2(byte - 127.0)
    codes = (blocks / scale).astype(np.float32).astype(dtype).astype(np.float64)
    return np.moveaxis((codes * scale).reshape(v.shape), -1, axis)


WIDE = False


def mx_kscale(k):
    if not WIDE:
        return np.ones(k)
    levels = np.array([10, -10, 5, -5, 0])
    a = np.random.permutation(np.resize(levels, k // 512 * 4)).reshape(k // 512, 4)
    idx = np.arange(k)
    return np.exp2(a[idx // 512, idx % 128 // 32])


BF16 = ml_dtypes.bfloat16


def bf(x):
    return np.asarray(x, np.float32).astype(BF16)


def f64(x):
    return np.asarray(x).astype(np.float64)


B, S, D, H = 2, 2048, 1024, 8
DH = D // H


def softmax(v, axis):
    e = np.exp(v - v.max(axis, keepdims=True))
    return e / e.sum(axis, keepdims=True)


def setup_inputs():
    s = mx_kscale(D)
    return {"x_k": bf(np.random.standard_normal((B, S, D)) * s),
            "W_K": bf(np.random.standard_normal((H, D, DH)) * 1.5 * DH ** 0.25 / np.sqrt(D) / s[:, None]),
            "v_heads": bf(np.random.standard_normal((B, H, S, DH)) * 2.0)}


def reference(x_k, W_K, v_heads):
    k = mxq(f64(x_k), 2, "e4m3")[:, None] @ mxq(f64(W_K), 1, "e4m3")[None]
    kt = softmax(np.swapaxes(k, -1, -2) / DH ** 0.25, -2)
    return mxq(kt, 3, "e4m3") @ mxq(f64(v_heads), 2, "e4m3")

@@ -1,0 +1,296 @@
+from contextlib import ExitStack
+
+import concourse.mybir as mybir
+from concourse.masks import make_identity
+
+F32 = mybir.dt.float32
+BF16 = mybir.dt.bfloat16
+U32 = mybir.dt.uint32
+U8 = mybir.dt.uint8
+FP8X4 = mybir.dt.float8_e4m3fn_x4
+EXP = mybir.ActivationFunctionType.Exp
+MAX = mybir.AluOpType.max
+MULT = mybir.AluOpType.mult
+AXIS_X = mybir.AxisListType.X
+
+B, S, D, H, DH = 2, 2048, 1024, 8, 128
+P = 128
+PACK = 4
+K_PASS = P * PACK
+BANK = 512
+
+FEATURE_PASSES = D // K_PASS
+QUADS_PER_BATCH = S // K_PASS
+QUADS = B * QUADS_PER_BATCH
+TILES = QUADS * PACK
+K_BANKS = H * DH // BANK
+HEADS_PER_BANK = BANK // DH
+PIECES = PACK
+PIECE_HEADS = H // PIECES
+PIECE_COLS = PIECE_HEADS * DH
+
+SOFTMAX_SCALE = 1.0 / DH**0.25
+
+X_AHEAD = 3
+V_AHEAD = 1
+NORMALISE_BEHIND = PACK
+QUANTISE_P_BEHIND = NORMALISE_BEHIND + 1
+SUMMARY_BEHIND = QUANTISE_P_BEHIND + 1
+LOAD_AHEAD = 2
+
+FLOPS = 2 * B * S * D * H * DH + 2 * B * H * S * DH * DH
+
+
+def tile_mhla2_pa_t_kernel(tc, x_k, W_K, v_heads, out):
+    nc = tc.nc
+    with ExitStack() as ctx:
+        keep = ctx.enter_context(tc.tile_pool(name="keep", bufs=1))
+        x_rows = ctx.enter_context(tc.tile_pool(name="x_rows", bufs=3))
+        k_first_rows = ctx.enter_context(tc.tile_pool(name="k_first_rows", bufs=3))
+        grouped_pool = ctx.enter_context(tc.tile_pool(name="grouped", bufs=2))
+        x_grouped_pool = ctx.enter_context(tc.tile_pool(name="x_grouped", bufs=3))
+        x_mx = ctx.enter_context(tc.tile_pool(name="x_mx", bufs=4))
+        quad_mx = ctx.enter_context(tc.tile_pool(name="quad_mx", bufs=QUADS_PER_BATCH + 2))
+        exp_pool = ctx.enter_context(tc.tile_pool(name="exp", bufs=2))
+        stats = ctx.enter_context(tc.tile_pool(name="stats", bufs=3))
+        result_pool = ctx.enter_context(tc.tile_pool(name="result", bufs=4))
+        k_psum = ctx.enter_context(tc.psum_pool(name="k_psum", bufs=2 * K_BANKS))
+        t_psum = ctx.enter_context(tc.psum_pool(name="t_psum", bufs=2))
+        o_psum = ctx.enter_context(tc.psum_pool(name="o_psum", bufs=2))
+        ctx.enter_context(tc.manual_schedule())
+
+        x_raw, v_raw, v_grouped, v_codes, v_scales = {}, {}, {}, {}, {}
+        x_grouped, x_codes, x_scales, k_banks, shift = {}, {}, {}, {}, {}
+        exps, sums, inv_sums, p_grouped, p_codes, p_scales = {}, {}, {}, {}, {}, {}
+
+        def quad_rows(q):
+            first = (q % QUADS_PER_BATCH) * K_PASS
+            return q // QUADS_PER_BATCH, slice(first, first + K_PASS)
+
+        def load_k_first(rows, name):
+            raw = k_first_rows.tile([P, H, PACK, DH], BF16, name=name, tag="k_first")
+            nc.sync.dma_start(out=raw[:], in_=rows.rearrange("h (p t) c -> p h t c", t=PACK))
+            return raw
+
+        def regroup_head(copy, raw, grouped, h):
+            copy(
+                out=grouped[:, h].rearrange("p (c i) t -> p c t i", i=4),
+                in_=raw[:, h].rearrange("p t (c i) -> p c t i", i=4),
+            )
+
+        def new_grouped(name):
+            return grouped_pool.tile([P, H, DH, PACK], BF16, name=name, tag="grouped", align_bytes=64)
+
+        def new_quad_mx(name):
+            codes = quad_mx.tile([P, H * DH], U32, name=name + "_codes", tag=name + "_codes", align_bytes=64)
+            scales = quad_mx.tile([P, H * DH], U8, name=name + "_scales", tag=name + "_scales", align_bytes=64)
+            return codes, scales
+
+        def quantise_piece(grouped, codes, scales, piece):
+            heads = slice(piece * PIECE_HEADS, (piece + 1) * PIECE_HEADS)
+            cols = slice(piece * PIECE_COLS, (piece + 1) * PIECE_COLS)
+            nc.vector.quantize_mx(
+                out=codes[:, cols].bitcast(FP8X4),
+                scales=scales[:, cols],
+                in_=grouped[:, heads].rearrange("p h c t -> p (h c t)"),
+            )
+
+        def load_x(q):
+            b, rows = quad_rows(q)
+            x_raw[q] = x_rows.tile([P, PACK, D], BF16, name="x_raw", tag="x_raw")
+            nc.sync.dma_start(out=x_raw[q][:], in_=x_k[b, rows, :].rearrange("(p j) d -> p j d", j=PACK))
+
+        def transpose_x(t):
+            words = x_raw[t // PACK][:, t % PACK, :].bitcast(F32)
+            pass_words = K_PASS // 2
+            turned = t_psum.tile([P, FEATURE_PASSES, 2, P], F32, name="turned", tag="turned")
+            for g in range(FEATURE_PASSES):
+                for u in range(2):
+                    nc.tensor.transpose(
+                        turned[:, g, u, :],
+                        words[:, g * pass_words + u : (g + 1) * pass_words : 2],
+                        identity[:],
+                    )
+            x_grouped[t] = x_grouped_pool.tile(
+                [P, FEATURE_PASSES * P * PACK], BF16, name="x_grouped", tag="x_grouped", align_bytes=64
+            )
+            nc.scalar.copy(
+                out=x_grouped[t][:].bitcast(F32).rearrange("p (g r u) -> p g r u", g=FEATURE_PASSES, u=2),
+                in_=turned[:].rearrange("p g u r -> p g r u"),
+            )
+
+        def quantise_x(t):
+            x_codes[t] = x_mx.tile([P, FEATURE_PASSES * P], U32, name="x_codes", tag="x_codes", align_bytes=64)
+            x_scales[t] = x_mx.tile([P, FEATURE_PASSES * P], U8, name="x_scales", tag="x_scales", align_bytes=64)
+            nc.vector.quantize_mx(
+                out=x_codes[t][:].bitcast(FP8X4), scales=x_scales[t][:], in_=x_grouped[t][:]
+            )
+
+        def project(t):
+            k_banks[t] = []
+            for n in range(K_BANKS):
+                bank = k_psum.tile([P, BANK], F32, name="k_bank", tag="k_bank")
+                for g in range(FEATURE_PASSES):
+                    tokens = slice(g * P, (g + 1) * P)
+                    cols = slice(n * BANK, (n + 1) * BANK)
+                    nc.tensor.matmul_mx(
+                        out=bank[:],
+                        lhsT=x_codes[t][:, tokens].bitcast(FP8X4),
+                        lhsT_scale=x_scales[t][:, tokens],
+                        rhs=w_codes[:, g, cols].bitcast(FP8X4),
+                        rhs_scale=w_scales[:, g, cols],
+                        start=(g == 0),
+                        stop=(g == FEATURE_PASSES - 1),
+                    )
+                k_banks[t].append(bank)
+
+        def row_max(t):
+            largest = stats.tile([P, H], F32, name="largest", tag="largest")
+            for n in range(K_BANKS):
+                nc.vector.tensor_reduce(
+                    out=largest[:, n * HEADS_PER_BANK : (n + 1) * HEADS_PER_BANK],
+                    in_=k_banks[t][n][:].rearrange("p (h c) -> p h c", h=HEADS_PER_BANK),
+                    axis=AXIS_X,
+                    op=MAX,
+                )
+            shift[t] = stats.tile([P, H], F32, name="shift", tag="shift")
+            nc.vector.tensor_scalar_mul(out=shift[t][:], in0=largest[:], scalar1=-SOFTMAX_SCALE)
+
+        def exponentials(t):
+            q, j = t // PACK, t % PACK
+            if j == 0:
+                exps[q] = exp_pool.tile([P, PACK, H * DH], F32, name="exps", tag="exps")
+                sums[q] = stats.tile([P, H * PACK], F32, name="sums", tag="sums")
+            for h in range(H):
+                bank = k_banks[t][h // HEADS_PER_BANK]
+                first = (h % HEADS_PER_BANK) * DH
+                nc.scalar.activation(
+                    out=exps[q][:, j, h * DH : (h + 1) * DH],
+                    in_=bank[:, first : first + DH],
+                    func=EXP,
+                    bias=shift[t][:, h : h + 1],
+                    scale=SOFTMAX_SCALE,
+                    accum_out=sums[q][:, h * PACK + j : h * PACK + j + 1],
+                )
+
+        def normalise(q, piece):
+            if piece == 0:
+                inv_sums[q] = stats.tile([P, H * PACK], F32, name="inv_sums", tag="inv_sums")
+                nc.vector.reciprocal(out=inv_sums[q][:], in_=sums[q][:])
+                p_grouped[q] = grouped_pool.tile(
+                    [P, H, DH, PACK], BF16, name="p_grouped", tag="p_grouped", align_bytes=64
+                )
+            heads = slice(piece * PIECE_HEADS, (piece + 1) * PIECE_HEADS)
+            nc.vector.tensor_tensor(
+                out=p_grouped[q][:, heads],
+                in0=exps[q][:, :, piece * PIECE_COLS : (piece + 1) * PIECE_COLS].rearrange(
+                    "p j (h c) -> p h c j", h=PIECE_HEADS
+                ),
+                in1=inv_sums[q][:, piece * PIECE_HEADS * PACK : (piece + 1) * PIECE_HEADS * PACK]
+                .rearrange("p (h j) -> p h j", j=PACK)
+                .unsqueeze(2)
+                .to_broadcast([P, PIECE_HEADS, DH, PACK]),
+                op=MULT,
+            )
+
+        def quantise_p(q, piece):
+            if piece == 0:
+                p_codes[q], p_scales[q] = new_quad_mx("p")
+            quantise_piece(p_grouped[q], p_codes[q], p_scales[q], piece)
+
+        def load_v(q):
+            b, rows = quad_rows(q)
+            v_raw[q] = load_k_first(v_heads[b, :, rows, :], "v_raw")
+
+        def regroup_v(q, piece):
+            if piece == 0:
+                v_grouped[q] = new_grouped("v_grouped")
+            for h in range(piece * PIECE_HEADS, (piece + 1) * PIECE_HEADS):
+                regroup_head(nc.scalar.copy, v_raw[q], v_grouped[q], h)
+
+        def quantise_v(q, piece):
+            if piece == 0:
+                v_codes[q], v_scales[q] = new_quad_mx("v")
+            quantise_piece(v_grouped[q], v_codes[q], v_scales[q], piece)
+
+        def summarise(b, piece):
+            summary = o_psum.tile([P, PIECE_HEADS, DH], F32, name="summary", tag="summary")
+            for i in range(PIECE_HEADS):
+                h = piece * PIECE_HEADS + i
+                cols = slice(h * DH, (h + 1) * DH)
+                for n in range(QUADS_PER_BATCH):
+                    q = b * QUADS_PER_BATCH + n
+                    nc.tensor.matmul_mx(
+                        out=summary[:, i, :],
+                        lhsT=p_codes[q][:, cols].bitcast(FP8X4),
+                        lhsT_scale=p_scales[q][:, cols],
+                        rhs=v_codes[q][:, cols].bitcast(FP8X4),
+                        rhs_scale=v_scales[q][:, cols],
+                        start=(n == 0),
+                        stop=(n == QUADS_PER_BATCH - 1),
+                    )
+            result = result_pool.tile([P, PIECE_HEADS, DH], F32, name="result", tag="result")
+            nc.scalar.copy(out=result[:], in_=summary[:])
+            heads = slice(piece * PIECE_HEADS, (piece + 1) * PIECE_HEADS)
+            nc.sync.dma_start(out=out[b, heads].rearrange("h c e -> c h e"), in_=result[:])
+
+        w_raw = [load_k_first(W_K[:, 0:K_PASS, :], "w_raw")]
+        load_x(0)
+        w_raw.append(load_k_first(W_K[:, K_PASS : 2 * K_PASS, :], "w_raw"))
+        load_v(0)
+        load_x(1)
+        load_v(1)
+
+        identity = keep.tile([P, P], F32, name="identity")
+        make_identity(nc, identity[:])
+        zero = keep.tile([P, 1], F32, name="zero")
+        one = keep.tile([P, 1], F32, name="one")
+        nc.vector.memset(zero[:], 0.0)
+        nc.scalar.activation(out=one[:], in_=zero[:], func=EXP)
+
+        w_codes = keep.tile([P, FEATURE_PASSES, H * DH], U32, name="w_codes", align_bytes=64)
+        w_scales = keep.tile([P, FEATURE_PASSES, H * DH], U8, name="w_scales", align_bytes=64)
+        w_grouped = []
+        for g in range(FEATURE_PASSES):
+            w_grouped.append(new_grouped("w_grouped"))
+            for h in range(H):
+                copy = nc.scalar.copy if h % 3 == 2 else nc.vector.tensor_copy
+                regroup_head(copy, w_raw[g], w_grouped[g], h)
+        for g in range(FEATURE_PASSES):
+            nc.vector.quantize_mx(
+                out=w_codes[:, g, :].bitcast(FP8X4),
+                scales=w_scales[:, g, :],
+                in_=w_grouped[g][:].rearrange("p h c t -> p (h c t)"),
+            )
+
+        def in_stream(index):
+            return 0 <= index < TILES
+
+        for slot in range(-X_AHEAD, TILES + SUMMARY_BEHIND):
+            if slot >= 0 and slot % PACK == 0 and slot // PACK + LOAD_AHEAD < QUADS:
+                load_x(slot // PACK + LOAD_AHEAD)
+                load_v(slot // PACK + LOAD_AHEAD)
+
+            if in_stream(slot + X_AHEAD):
+                transpose_x(slot + X_AHEAD)
+            if in_stream(slot + 1):
+                project(slot + 1)
+            if in_stream(slot):
+                row_max(slot)
+            if in_stream(slot + V_AHEAD):
+                regroup_v((slot + V_AHEAD) // PACK, (slot + V_AHEAD) % PACK)
+            if in_stream(slot):
+                exponentials(slot)
+
+            done = slot - SUMMARY_BEHIND
+            if in_stream(done) and (done // PACK) % QUADS_PER_BATCH == QUADS_PER_BATCH - 1:
+                summarise(done // PACK // QUADS_PER_BATCH, done % PACK)
+
+            if in_stream(slot - NORMALISE_BEHIND):
+                normalise((slot - NORMALISE_BEHIND) // PACK, (slot - NORMALISE_BEHIND) % PACK)
+            if in_stream(slot + X_AHEAD - 1):
+                quantise_x(slot + X_AHEAD - 1)
+            if in_stream(slot + V_AHEAD - 1):
+                quantise_v((slot + V_AHEAD - 1) // PACK, (slot + V_AHEAD - 1) % PACK)
+            if in_stream(slot - QUANTISE_P_BEHIND):
+                quantise_p((slot - QUANTISE_P_BEHIND) // PACK, (slot - QUANTISE_P_BEHIND) % PACK)

@@ -11,6 +11,7 @@ FP8X4 = mybir.dt.float8_e4m3fn_x4
 EXP = mybir.ActivationFunctionType.Exp
 MAX = mybir.AluOpType.max
 MULT = mybir.AluOpType.mult
+ADD = mybir.AluOpType.add
 AXIS_X = mybir.AxisListType.X
 
 B, S, D, H, DH = 2, 2048, 1024, 8, 128
@@ -32,11 +33,13 @@ PIECE_COLS = PIECE_HEADS * DH
 SOFTMAX_SCALE = 1.0 / DH**0.25
 
 X_AHEAD = 3
-V_AHEAD = 1
+V_AHEAD = 2
 NORMALISE_BEHIND = PACK
 QUANTISE_P_BEHIND = NORMALISE_BEHIND + 1
 SUMMARY_BEHIND = QUANTISE_P_BEHIND + 1
-LOAD_AHEAD = 2
+X_LOAD_AHEAD = X_AHEAD + 4
+V_LOAD_AHEAD = V_AHEAD + 4
+FIRST_SLOT = -X_AHEAD
 
 FLOPS = 2 * B * S * D * H * DH + 2 * B * H * S * DH * DH
 
@@ -45,7 +48,7 @@ def tile_mhla2_pa_t_kernel(tc, x_k, W_K, v_heads, out):
     nc = tc.nc
     with ExitStack() as ctx:
         keep = ctx.enter_context(tc.tile_pool(name="keep", bufs=1))
-        x_rows = ctx.enter_context(tc.tile_pool(name="x_rows", bufs=3))
+        x_rows = ctx.enter_context(tc.tile_pool(name="x_rows", bufs=X_LOAD_AHEAD + 1))
         k_first_rows = ctx.enter_context(tc.tile_pool(name="k_first_rows", bufs=3))
         grouped_pool = ctx.enter_context(tc.tile_pool(name="grouped", bufs=2))
         x_grouped_pool = ctx.enter_context(tc.tile_pool(name="x_grouped", bufs=3))
@@ -95,13 +98,15 @@ def tile_mhla2_pa_t_kernel(tc, x_k, W_K, v_heads, out):
                 in_=grouped[:, heads].rearrange("p h c t -> p (h c t)"),
             )
 
-        def load_x(q):
-            b, rows = quad_rows(q)
-            x_raw[q] = x_rows.tile([P, PACK, D], BF16, name="x_raw", tag="x_raw")
-            nc.sync.dma_start(out=x_raw[q][:], in_=x_k[b, rows, :].rearrange("(p j) d -> p j d", j=PACK))
+        def load_x(t):
+            b, rows = quad_rows(t // PACK)
+            x_raw[t] = x_rows.tile([P, D], BF16, name="x_raw", tag="x_raw")
+            nc.sync.dma_start(
+                out=x_raw[t][:], in_=x_k[b, rows, :].rearrange("(p j) d -> p j d", j=PACK)[:, t % PACK, :]
+            )
 
         def transpose_x(t):
-            words = x_raw[t // PACK][:, t % PACK, :].bitcast(F32)
+            words = x_raw[t][:].bitcast(F32)
             pass_words = K_PASS // 2
             turned = t_psum.tile([P, FEATURE_PASSES, 2, P], F32, name="turned", tag="turned")
             for g in range(FEATURE_PASSES):
@@ -176,17 +181,18 @@ def tile_mhla2_pa_t_kernel(tc, x_k, W_K, v_heads, out):
         def normalise(q, piece):
             if piece == 0:
                 inv_sums[q] = stats.tile([P, H * PACK], F32, name="inv_sums", tag="inv_sums")
-                nc.vector.reciprocal(out=inv_sums[q][:], in_=sums[q][:])
                 p_grouped[q] = grouped_pool.tile(
                     [P, H, DH, PACK], BF16, name="p_grouped", tag="p_grouped", align_bytes=64
                 )
             heads = slice(piece * PIECE_HEADS, (piece + 1) * PIECE_HEADS)
+            piece_sums = slice(piece * PIECE_HEADS * PACK, (piece + 1) * PIECE_HEADS * PACK)
+            nc.vector.reciprocal(out=inv_sums[q][:, piece_sums], in_=sums[q][:, piece_sums])
             nc.vector.tensor_tensor(
                 out=p_grouped[q][:, heads],
                 in0=exps[q][:, :, piece * PIECE_COLS : (piece + 1) * PIECE_COLS].rearrange(
                     "p j (h c) -> p h c j", h=PIECE_HEADS
                 ),
-                in1=inv_sums[q][:, piece * PIECE_HEADS * PACK : (piece + 1) * PIECE_HEADS * PACK]
+                in1=inv_sums[q][:, piece_sums]
                 .rearrange("p (h j) -> p h j", j=PACK)
                 .unsqueeze(2)
                 .to_broadcast([P, PIECE_HEADS, DH, PACK]),
@@ -205,8 +211,16 @@ def tile_mhla2_pa_t_kernel(tc, x_k, W_K, v_heads, out):
         def regroup_v(q, piece):
             if piece == 0:
                 v_grouped[q] = new_grouped("v_grouped")
-            for h in range(piece * PIECE_HEADS, (piece + 1) * PIECE_HEADS):
-                regroup_head(nc.scalar.copy, v_raw[q], v_grouped[q], h)
+            regroup_head(nc.scalar.copy, v_raw[q], v_grouped[q], piece * PIECE_HEADS)
+            h = piece * PIECE_HEADS + 1
+            nc.gpsimd.tensor_scalar(
+                out=v_grouped[q][:, h],
+                in0=v_raw[q][:, h].rearrange("p t c -> p c t"),
+                scalar1=1.0,
+                scalar2=0.0,
+                op0=MULT,
+                op1=ADD,
+            )
 
         def quantise_v(q, piece):
             if piece == 0:
@@ -234,12 +248,11 @@ def tile_mhla2_pa_t_kernel(tc, x_k, W_K, v_heads, out):
             heads = slice(piece * PIECE_HEADS, (piece + 1) * PIECE_HEADS)
             nc.sync.dma_start(out=out[b, heads].rearrange("h c e -> c h e"), in_=result[:])
 
-        w_raw = [load_k_first(W_K[:, 0:K_PASS, :], "w_raw")]
         load_x(0)
-        w_raw.append(load_k_first(W_K[:, K_PASS : 2 * K_PASS, :], "w_raw"))
+        w_raw = [load_k_first(W_K[:, g * K_PASS : (g + 1) * K_PASS, :], "w_raw") for g in range(FEATURE_PASSES)]
+        for t in range(1, FIRST_SLOT + X_LOAD_AHEAD):
+            load_x(t)
         load_v(0)
-        load_x(1)
-        load_v(1)
 
         identity = keep.tile([P, P], F32, name="identity")
         make_identity(nc, identity[:])
@@ -250,26 +263,29 @@ def tile_mhla2_pa_t_kernel(tc, x_k, W_K, v_heads, out):
 
         w_codes = keep.tile([P, FEATURE_PASSES, H * DH], U32, name="w_codes", align_bytes=64)
         w_scales = keep.tile([P, FEATURE_PASSES, H * DH], U8, name="w_scales", align_bytes=64)
-        w_grouped = []
-        for g in range(FEATURE_PASSES):
-            w_grouped.append(new_grouped("w_grouped"))
-            for h in range(H):
-                copy = nc.scalar.copy if h % 3 == 2 else nc.vector.tensor_copy
-                regroup_head(copy, w_raw[g], w_grouped[g], h)
-        for g in range(FEATURE_PASSES):
-            nc.vector.quantize_mx(
-                out=w_codes[:, g, :].bitcast(FP8X4),
-                scales=w_scales[:, g, :],
-                in_=w_grouped[g][:].rearrange("p h c t -> p (h c t)"),
-            )
+
+        def prepare_w():
+            for g in range(FEATURE_PASSES):
+                w_grouped = new_grouped("w_grouped")
+                for h in range(H):
+                    copy = nc.scalar.copy if h % 3 == 2 else nc.vector.tensor_copy
+                    regroup_head(copy, w_raw[g], w_grouped, h)
+                nc.vector.quantize_mx(
+                    out=w_codes[:, g, :].bitcast(FP8X4),
+                    scales=w_scales[:, g, :],
+                    in_=w_grouped[:].rearrange("p h c t -> p (h c t)"),
+                )
 
         def in_stream(index):
             return 0 <= index < TILES
 
-        for slot in range(-X_AHEAD, TILES + SUMMARY_BEHIND):
-            if slot >= 0 and slot % PACK == 0 and slot // PACK + LOAD_AHEAD < QUADS:
-                load_x(slot // PACK + LOAD_AHEAD)
-                load_v(slot // PACK + LOAD_AHEAD)
+        for slot in range(FIRST_SLOT, TILES + SUMMARY_BEHIND):
+            if slot == FIRST_SLOT + 1:
+                prepare_w()
+            if in_stream(slot + X_LOAD_AHEAD):
+                load_x(slot + X_LOAD_AHEAD)
+            if 0 < slot + V_LOAD_AHEAD < TILES and (slot + V_LOAD_AHEAD) % PACK == 0:
+                load_v((slot + V_LOAD_AHEAD) // PACK)
 
             if in_stream(slot + X_AHEAD):
                 transpose_x(slot + X_AHEAD)
@@ -288,9 +304,9 @@ def tile_mhla2_pa_t_kernel(tc, x_k, W_K, v_heads, out):
 
             if in_stream(slot - NORMALISE_BEHIND):
                 normalise((slot - NORMALISE_BEHIND) // PACK, (slot - NORMALISE_BEHIND) % PACK)
-            if in_stream(slot + X_AHEAD - 1):
-                quantise_x(slot + X_AHEAD - 1)
-            if in_stream(slot + V_AHEAD - 1):
-                quantise_v((slot + V_AHEAD - 1) // PACK, (slot + V_AHEAD - 1) % PACK)
+            if in_stream(slot + X_AHEAD):
+                quantise_x(slot + X_AHEAD)
+            if in_stream(slot):
+                quantise_v(slot // PACK, slot % PACK)
             if in_stream(slot - QUANTISE_P_BEHIND):
                 quantise_p((slot - QUANTISE_P_BEHIND) // PACK, (slot - QUANTISE_P_BEHIND) % PACK)

@@ -11,7 +11,6 @@ FP8X4 = mybir.dt.float8_e4m3fn_x4
 EXP = mybir.ActivationFunctionType.Exp
 MAX = mybir.AluOpType.max
 MULT = mybir.AluOpType.mult
-ADD = mybir.AluOpType.add
 AXIS_X = mybir.AxisListType.X
 
 B, S, D, H, DH = 2, 2048, 1024, 8, 128
@@ -33,13 +32,11 @@ PIECE_COLS = PIECE_HEADS * DH
 SOFTMAX_SCALE = 1.0 / DH**0.25
 
 X_AHEAD = 3
-V_AHEAD = 2
+V_AHEAD = 1
 NORMALISE_BEHIND = PACK
 QUANTISE_P_BEHIND = NORMALISE_BEHIND + 1
 SUMMARY_BEHIND = QUANTISE_P_BEHIND + 1
-X_LOAD_AHEAD = X_AHEAD + 4
-V_LOAD_AHEAD = V_AHEAD + 4
-FIRST_SLOT = -X_AHEAD
+LOAD_AHEAD = 2
 
 FLOPS = 2 * B * S * D * H * DH + 2 * B * H * S * DH * DH
 
@@ -48,7 +45,7 @@ def tile_mhla2_pa_t_kernel(tc, x_k, W_K, v_heads, out):
     nc = tc.nc
     with ExitStack() as ctx:
         keep = ctx.enter_context(tc.tile_pool(name="keep", bufs=1))
-        x_rows = ctx.enter_context(tc.tile_pool(name="x_rows", bufs=X_LOAD_AHEAD + 1))
+        x_rows = ctx.enter_context(tc.tile_pool(name="x_rows", bufs=3))
         k_first_rows = ctx.enter_context(tc.tile_pool(name="k_first_rows", bufs=3))
         grouped_pool = ctx.enter_context(tc.tile_pool(name="grouped", bufs=2))
         x_grouped_pool = ctx.enter_context(tc.tile_pool(name="x_grouped", bufs=3))
@@ -60,7 +57,6 @@ def tile_mhla2_pa_t_kernel(tc, x_k, W_K, v_heads, out):
         k_psum = ctx.enter_context(tc.psum_pool(name="k_psum", bufs=2 * K_BANKS))
         t_psum = ctx.enter_context(tc.psum_pool(name="t_psum", bufs=2))
         o_psum = ctx.enter_context(tc.psum_pool(name="o_psum", bufs=2))
-        ctx.enter_context(tc.manual_schedule())
 
         x_raw, v_raw, v_grouped, v_codes, v_scales = {}, {}, {}, {}, {}
         x_grouped, x_codes, x_scales, k_banks, shift = {}, {}, {}, {}, {}
@@ -98,15 +94,13 @@ def tile_mhla2_pa_t_kernel(tc, x_k, W_K, v_heads, out):
                 in_=grouped[:, heads].rearrange("p h c t -> p (h c t)"),
             )
 
-        def load_x(t):
-            b, rows = quad_rows(t // PACK)
-            x_raw[t] = x_rows.tile([P, D], BF16, name="x_raw", tag="x_raw")
-            nc.sync.dma_start(
-                out=x_raw[t][:], in_=x_k[b, rows, :].rearrange("(p j) d -> p j d", j=PACK)[:, t % PACK, :]
-            )
+        def load_x(q):
+            b, rows = quad_rows(q)
+            x_raw[q] = x_rows.tile([P, PACK, D], BF16, name="x_raw", tag="x_raw")
+            nc.sync.dma_start(out=x_raw[q][:], in_=x_k[b, rows, :].rearrange("(p j) d -> p j d", j=PACK))
 
         def transpose_x(t):
-            words = x_raw[t][:].bitcast(F32)
+            words = x_raw[t // PACK][:, t % PACK, :].bitcast(F32)
             pass_words = K_PASS // 2
             turned = t_psum.tile([P, FEATURE_PASSES, 2, P], F32, name="turned", tag="turned")
             for g in range(FEATURE_PASSES):
@@ -181,18 +175,17 @@ def tile_mhla2_pa_t_kernel(tc, x_k, W_K, v_heads, out):
         def normalise(q, piece):
             if piece == 0:
                 inv_sums[q] = stats.tile([P, H * PACK], F32, name="inv_sums", tag="inv_sums")
+                nc.vector.reciprocal(out=inv_sums[q][:], in_=sums[q][:])
                 p_grouped[q] = grouped_pool.tile(
                     [P, H, DH, PACK], BF16, name="p_grouped", tag="p_grouped", align_bytes=64
                 )
             heads = slice(piece * PIECE_HEADS, (piece + 1) * PIECE_HEADS)
-            piece_sums = slice(piece * PIECE_HEADS * PACK, (piece + 1) * PIECE_HEADS * PACK)
-            nc.vector.reciprocal(out=inv_sums[q][:, piece_sums], in_=sums[q][:, piece_sums])
             nc.vector.tensor_tensor(
                 out=p_grouped[q][:, heads],
                 in0=exps[q][:, :, piece * PIECE_COLS : (piece + 1) * PIECE_COLS].rearrange(
                     "p j (h c) -> p h c j", h=PIECE_HEADS
                 ),
-                in1=inv_sums[q][:, piece_sums]
+                in1=inv_sums[q][:, piece * PIECE_HEADS * PACK : (piece + 1) * PIECE_HEADS * PACK]
                 .rearrange("p (h j) -> p h j", j=PACK)
                 .unsqueeze(2)
                 .to_broadcast([P, PIECE_HEADS, DH, PACK]),
@@ -211,16 +204,8 @@ def tile_mhla2_pa_t_kernel(tc, x_k, W_K, v_heads, out):
         def regroup_v(q, piece):
             if piece == 0:
                 v_grouped[q] = new_grouped("v_grouped")
-            regroup_head(nc.scalar.copy, v_raw[q], v_grouped[q], piece * PIECE_HEADS)
-            h = piece * PIECE_HEADS + 1
-            nc.gpsimd.tensor_scalar(
-                out=v_grouped[q][:, h],
-                in0=v_raw[q][:, h].rearrange("p t c -> p c t"),
-                scalar1=1.0,
-                scalar2=0.0,
-                op0=MULT,
-                op1=ADD,
-            )
+            for h in range(piece * PIECE_HEADS, (piece + 1) * PIECE_HEADS):
+                regroup_head(nc.scalar.copy, v_raw[q], v_grouped[q], h)
 
         def quantise_v(q, piece):
             if piece == 0:
@@ -248,11 +233,12 @@ def tile_mhla2_pa_t_kernel(tc, x_k, W_K, v_heads, out):
             heads = slice(piece * PIECE_HEADS, (piece + 1) * PIECE_HEADS)
             nc.sync.dma_start(out=out[b, heads].rearrange("h c e -> c h e"), in_=result[:])
 
+        w_raw = [load_k_first(W_K[:, 0:K_PASS, :], "w_raw")]
         load_x(0)
-        w_raw = [load_k_first(W_K[:, g * K_PASS : (g + 1) * K_PASS, :], "w_raw") for g in range(FEATURE_PASSES)]
-        for t in range(1, FIRST_SLOT + X_LOAD_AHEAD):
-            load_x(t)
+        w_raw.append(load_k_first(W_K[:, K_PASS : 2 * K_PASS, :], "w_raw"))
         load_v(0)
+        load_x(1)
+        load_v(1)
 
         identity = keep.tile([P, P], F32, name="identity")
         make_identity(nc, identity[:])
@@ -263,29 +249,26 @@ def tile_mhla2_pa_t_kernel(tc, x_k, W_K, v_heads, out):
 
         w_codes = keep.tile([P, FEATURE_PASSES, H * DH], U32, name="w_codes", align_bytes=64)
         w_scales = keep.tile([P, FEATURE_PASSES, H * DH], U8, name="w_scales", align_bytes=64)
-
-        def prepare_w():
-            for g in range(FEATURE_PASSES):
-                w_grouped = new_grouped("w_grouped")
-                for h in range(H):
-                    copy = nc.scalar.copy if h % 3 == 2 else nc.vector.tensor_copy
-                    regroup_head(copy, w_raw[g], w_grouped, h)
-                nc.vector.quantize_mx(
-                    out=w_codes[:, g, :].bitcast(FP8X4),
-                    scales=w_scales[:, g, :],
-                    in_=w_grouped[:].rearrange("p h c t -> p (h c t)"),
-                )
+        w_grouped = []
+        for g in range(FEATURE_PASSES):
+            w_grouped.append(new_grouped("w_grouped"))
+            for h in range(H):
+                copy = nc.scalar.copy if h % 3 == 2 else nc.vector.tensor_copy
+                regroup_head(copy, w_raw[g], w_grouped[g], h)
+        for g in range(FEATURE_PASSES):
+            nc.vector.quantize_mx(
+                out=w_codes[:, g, :].bitcast(FP8X4),
+                scales=w_scales[:, g, :],
+                in_=w_grouped[g][:].rearrange("p h c t -> p (h c t)"),
+            )
 
         def in_stream(index):
             return 0 <= index < TILES
 
-        for slot in range(FIRST_SLOT, TILES + SUMMARY_BEHIND):
-            if slot == FIRST_SLOT + 1:
-                prepare_w()
-            if in_stream(slot + X_LOAD_AHEAD):
-                load_x(slot + X_LOAD_AHEAD)
-            if 0 < slot + V_LOAD_AHEAD < TILES and (slot + V_LOAD_AHEAD) % PACK == 0:
-                load_v((slot + V_LOAD_AHEAD) // PACK)
+        for slot in range(-X_AHEAD, TILES + SUMMARY_BEHIND):
+            if slot >= 0 and slot % PACK == 0 and slot // PACK + LOAD_AHEAD < QUADS:
+                load_x(slot // PACK + LOAD_AHEAD)
+                load_v(slot // PACK + LOAD_AHEAD)
 
             if in_stream(slot + X_AHEAD):
                 transpose_x(slot + X_AHEAD)
@@ -304,9 +287,9 @@ def tile_mhla2_pa_t_kernel(tc, x_k, W_K, v_heads, out):
 
             if in_stream(slot - NORMALISE_BEHIND):
                 normalise((slot - NORMALISE_BEHIND) // PACK, (slot - NORMALISE_BEHIND) % PACK)
-            if in_stream(slot + X_AHEAD):
-                quantise_x(slot + X_AHEAD)
-            if in_stream(slot):
-                quantise_v(slot // PACK, slot % PACK)
+            if in_stream(slot + X_AHEAD - 1):
+                quantise_x(slot + X_AHEAD - 1)
+            if in_stream(slot + V_AHEAD - 1):
+                quantise_v((slot + V_AHEAD - 1) // PACK, (slot + V_AHEAD - 1) % PACK)
             if in_stream(slot - QUANTISE_P_BEHIND):
                 quantise_p((slot - QUANTISE_P_BEHIND) // PACK, (slot - QUANTISE_P_BEHIND) % PACK)

@@ -153,7 +153,7 @@ def tile_mhla2_pa_t_kernel(tc, x_k, W_K, v_heads, out):
                     op=MAX,
                 )
             shift[t] = stats.tile([P, H], F32, name="shift", tag="shift")
-            nc.vector.tensor_scalar_mul(out=shift[t][:], in0=largest[:], scalar1=-SOFTMAX_SCALE)
+            nc.scalar.mul(out=shift[t][:], in_=largest[:], mul=-SOFTMAX_SCALE)
 
         def exponentials(t):
             q, j = t // PACK, t % PACK
@@ -179,18 +179,16 @@ def tile_mhla2_pa_t_kernel(tc, x_k, W_K, v_heads, out):
                 p_grouped[q] = grouped_pool.tile(
                     [P, H, DH, PACK], BF16, name="p_grouped", tag="p_grouped", align_bytes=64
                 )
-            heads = slice(piece * PIECE_HEADS, (piece + 1) * PIECE_HEADS)
-            nc.vector.tensor_tensor(
-                out=p_grouped[q][:, heads],
-                in0=exps[q][:, :, piece * PIECE_COLS : (piece + 1) * PIECE_COLS].rearrange(
-                    "p j (h c) -> p h c j", h=PIECE_HEADS
-                ),
-                in1=inv_sums[q][:, piece * PIECE_HEADS * PACK : (piece + 1) * PIECE_HEADS * PACK]
-                .rearrange("p (h j) -> p h j", j=PACK)
-                .unsqueeze(2)
-                .to_broadcast([P, PIECE_HEADS, DH, PACK]),
-                op=MULT,
-            )
+            for h in range(piece * PIECE_HEADS, (piece + 1) * PIECE_HEADS):
+                nc.vector.tensor_tensor(
+                    out=p_grouped[q][:, h].rearrange("p (c i) j -> p c j i", i=4),
+                    in0=exps[q][:, :, h * DH : (h + 1) * DH].rearrange("p j (c i) -> p c j i", i=4),
+                    in1=inv_sums[q][:, h * PACK : (h + 1) * PACK]
+                    .unsqueeze(1)
+                    .unsqueeze(3)
+                    .to_broadcast([P, DH // 4, PACK, 4]),
+                    op=MULT,
+                )
 
         def quantise_p(q, piece):
             if piece == 0:
@@ -207,10 +205,13 @@ def tile_mhla2_pa_t_kernel(tc, x_k, W_K, v_heads, out):
             for h in range(piece * PIECE_HEADS, (piece + 1) * PIECE_HEADS):
                 regroup_head(nc.scalar.copy, v_raw[q], v_grouped[q], h)
 
-        def quantise_v(q, piece):
-            if piece == 0:
-                v_codes[q], v_scales[q] = new_quad_mx("v")
-            quantise_piece(v_grouped[q], v_codes[q], v_scales[q], piece)
+        def quantise_v(q):
+            v_codes[q], v_scales[q] = new_quad_mx("v")
+            nc.vector.quantize_mx(
+                out=v_codes[q][:].bitcast(FP8X4),
+                scales=v_scales[q][:],
+                in_=v_grouped[q][:].rearrange("p h c t -> p (h c t)"),
+            )
 
         def summarise(b, piece):
             summary = o_psum.tile([P, PIECE_HEADS, DH], F32, name="summary", tag="summary")
@@ -289,7 +290,7 @@ def tile_mhla2_pa_t_kernel(tc, x_k, W_K, v_heads, out):
                 normalise((slot - NORMALISE_BEHIND) // PACK, (slot - NORMALISE_BEHIND) % PACK)
             if in_stream(slot + X_AHEAD - 1):
                 quantise_x(slot + X_AHEAD - 1)
-            if in_stream(slot + V_AHEAD - 1):
-                quantise_v((slot + V_AHEAD - 1) // PACK, (slot + V_AHEAD - 1) % PACK)
+            if in_stream(slot + V_AHEAD - 1) and (slot + V_AHEAD - 1) % PACK == PACK - 1:
+                quantise_v((slot + V_AHEAD - 1) // PACK)
             if in_stream(slot - QUANTISE_P_BEHIND):
                 quantise_p((slot - QUANTISE_P_BEHIND) // PACK, (slot - QUANTISE_P_BEHIND) % PACK)

@@ -179,16 +179,18 @@ def tile_mhla2_pa_t_kernel(tc, x_k, W_K, v_heads, out):
                 p_grouped[q] = grouped_pool.tile(
                     [P, H, DH, PACK], BF16, name="p_grouped", tag="p_grouped", align_bytes=64
                 )
-            for h in range(piece * PIECE_HEADS, (piece + 1) * PIECE_HEADS):
-                nc.vector.tensor_tensor(
-                    out=p_grouped[q][:, h].rearrange("p (c i) j -> p c j i", i=4),
-                    in0=exps[q][:, :, h * DH : (h + 1) * DH].rearrange("p j (c i) -> p c j i", i=4),
-                    in1=inv_sums[q][:, h * PACK : (h + 1) * PACK]
-                    .unsqueeze(1)
-                    .unsqueeze(3)
-                    .to_broadcast([P, DH // 4, PACK, 4]),
-                    op=MULT,
-                )
+            heads = slice(piece * PIECE_HEADS, (piece + 1) * PIECE_HEADS)
+            nc.vector.tensor_tensor(
+                out=p_grouped[q][:, heads],
+                in0=exps[q][:, :, piece * PIECE_COLS : (piece + 1) * PIECE_COLS].rearrange(
+                    "p j (h c) -> p h c j", h=PIECE_HEADS
+                ),
+                in1=inv_sums[q][:, piece * PIECE_HEADS * PACK : (piece + 1) * PIECE_HEADS * PACK]
+                .rearrange("p (h j) -> p h j", j=PACK)
+                .unsqueeze(2)
+                .to_broadcast([P, PIECE_HEADS, DH, PACK]),
+                op=MULT,
+            )
 
         def quantise_p(q, piece):
             if piece == 0:

@@ -68,7 +68,9 @@ def tile_mhla2_pa_t_kernel(tc, x_k, W_K, v_heads, out):
 
         def load_k_first(rows, name):
             raw = k_first_rows.tile([P, H, PACK, DH], BF16, name=name, tag="k_first")
-            nc.sync.dma_start(out=raw[:], in_=rows.rearrange("h (p t) c -> p h t c", t=PACK))
+            for piece in range(PIECES):
+                heads = slice(piece * PIECE_HEADS, (piece + 1) * PIECE_HEADS)
+                nc.sync.dma_start(out=raw[:, heads], in_=rows[heads].rearrange("h (p t) c -> p h t c", t=PACK))
             return raw
 
         def regroup_head(copy, raw, grouped, h):
@@ -179,18 +181,16 @@ def tile_mhla2_pa_t_kernel(tc, x_k, W_K, v_heads, out):
                 p_grouped[q] = grouped_pool.tile(
                     [P, H, DH, PACK], BF16, name="p_grouped", tag="p_grouped", align_bytes=64
                 )
-            heads = slice(piece * PIECE_HEADS, (piece + 1) * PIECE_HEADS)
-            nc.vector.tensor_tensor(
-                out=p_grouped[q][:, heads],
-                in0=exps[q][:, :, piece * PIECE_COLS : (piece + 1) * PIECE_COLS].rearrange(
-                    "p j (h c) -> p h c j", h=PIECE_HEADS
-                ),
-                in1=inv_sums[q][:, piece * PIECE_HEADS * PACK : (piece + 1) * PIECE_HEADS * PACK]
-                .rearrange("p (h j) -> p h j", j=PACK)
-                .unsqueeze(2)
-                .to_broadcast([P, PIECE_HEADS, DH, PACK]),
-                op=MULT,
-            )
+            for h in range(piece * PIECE_HEADS, (piece + 1) * PIECE_HEADS):
+                nc.vector.tensor_tensor(
+                    out=p_grouped[q][:, h].rearrange("p (c i) j -> p c j i", i=4),
+                    in0=exps[q][:, :, h * DH : (h + 1) * DH].rearrange("p j (c i) -> p c j i", i=4),
+                    in1=inv_sums[q][:, h * PACK : (h + 1) * PACK]
+                    .unsqueeze(1)
+                    .unsqueeze(3)
+                    .to_broadcast([P, DH // 4, PACK, 4]),
+                    op=MULT,
+                )
 
         def quantise_p(q, piece):
             if piece == 0:

@@ -11,6 +11,7 @@ FP8X4 = mybir.dt.float8_e4m3fn_x4
 EXP = mybir.ActivationFunctionType.Exp
 MAX = mybir.AluOpType.max
 MULT = mybir.AluOpType.mult
+ADD = mybir.AluOpType.add
 AXIS_X = mybir.AxisListType.X
 
 B, S, D, H, DH = 2, 2048, 1024, 8, 128
@@ -23,17 +24,21 @@ FEATURE_PASSES = D // K_PASS
 QUADS_PER_BATCH = S // K_PASS
 QUADS = B * QUADS_PER_BATCH
 TILES = QUADS * PACK
-K_BANKS = H * DH // BANK
-HEADS_PER_BANK = BANK // DH
-PIECES = PACK
-PIECE_HEADS = H // PIECES
+HALVES = H * DH // BANK
+HALF_HEADS = H // HALVES
+SLOT_TILES = 2
+GROUP_SLOTS = PACK // SLOT_TILES
+GROUPS = QUADS * HALVES
+SLOTS = GROUPS * GROUP_SLOTS
+QUAD_SLOTS = HALVES * GROUP_SLOTS
+PIECE_HEADS = H // QUAD_SLOTS
 PIECE_COLS = PIECE_HEADS * DH
 
 SOFTMAX_SCALE = 1.0 / DH**0.25
 
-X_AHEAD = 3
+X_AHEAD = 6
 V_AHEAD = 1
-NORMALISE_BEHIND = PACK
+NORMALISE_BEHIND = GROUP_SLOTS + 1
 QUANTISE_P_BEHIND = NORMALISE_BEHIND + 1
 SUMMARY_BEHIND = QUANTISE_P_BEHIND + 1
 LOAD_AHEAD = 2
@@ -45,42 +50,38 @@ def tile_mhla2_pa_t_kernel(tc, x_k, W_K, v_heads, out):
     nc = tc.nc
     with ExitStack() as ctx:
         keep = ctx.enter_context(tc.tile_pool(name="keep", bufs=1))
-        x_rows = ctx.enter_context(tc.tile_pool(name="x_rows", bufs=3))
+        x_rows = ctx.enter_context(tc.tile_pool(name="x_rows", bufs=4))
         k_first_rows = ctx.enter_context(tc.tile_pool(name="k_first_rows", bufs=3))
+        w_pool = ctx.enter_context(tc.tile_pool(name="w_pool", bufs=4))
         grouped_pool = ctx.enter_context(tc.tile_pool(name="grouped", bufs=2))
-        x_grouped_pool = ctx.enter_context(tc.tile_pool(name="x_grouped", bufs=3))
-        x_mx = ctx.enter_context(tc.tile_pool(name="x_mx", bufs=4))
+        x_grouped_pool = ctx.enter_context(tc.tile_pool(name="x_grouped", bufs=2))
+        x_mx = ctx.enter_context(tc.tile_pool(name="x_mx", bufs=5))
         quad_mx = ctx.enter_context(tc.tile_pool(name="quad_mx", bufs=QUADS_PER_BATCH + 2))
-        exp_pool = ctx.enter_context(tc.tile_pool(name="exp", bufs=2))
-        stats = ctx.enter_context(tc.tile_pool(name="stats", bufs=3))
+        exp_pool = ctx.enter_context(tc.tile_pool(name="exp", bufs=3))
+        stats = ctx.enter_context(tc.tile_pool(name="stats", bufs=4))
         result_pool = ctx.enter_context(tc.tile_pool(name="result", bufs=4))
-        k_psum = ctx.enter_context(tc.psum_pool(name="k_psum", bufs=2 * K_BANKS))
+        k_psum = ctx.enter_context(tc.psum_pool(name="k_psum", bufs=4))
         t_psum = ctx.enter_context(tc.psum_pool(name="t_psum", bufs=2))
-        o_psum = ctx.enter_context(tc.psum_pool(name="o_psum", bufs=2))
+        o_psum = ctx.enter_context(tc.psum_pool(name="o_psum", bufs=1))
+        i_psum = ctx.enter_context(tc.psum_pool(name="i_psum", bufs=1))
 
-        x_raw, v_raw, v_grouped, v_codes, v_scales = {}, {}, {}, {}, {}
-        x_grouped, x_codes, x_scales, k_banks, shift = {}, {}, {}, {}, {}
-        exps, sums, inv_sums, p_grouped, p_codes, p_scales = {}, {}, {}, {}, {}, {}
+        x_raw, turned_x, v_raw, v_grouped, v_codes, v_scales = {}, {}, {}, {}, {}, {}
+        x_grouped, x_codes, x_scales, k_banks, largest, shift = {}, {}, {}, {}, {}, {}
+        exps, sums, inv_sums, inv_banks, p_grouped, p_codes, p_scales = {}, {}, {}, {}, {}, {}, {}
+        w_grouped = {}
 
         def quad_rows(q):
             first = (q % QUADS_PER_BATCH) * K_PASS
             return q // QUADS_PER_BATCH, slice(first, first + K_PASS)
 
-        def load_k_first(rows, name):
-            raw = k_first_rows.tile([P, H, PACK, DH], BF16, name=name, tag="k_first")
-            for piece in range(PIECES):
-                heads = slice(piece * PIECE_HEADS, (piece + 1) * PIECE_HEADS)
-                nc.sync.dma_start(out=raw[:, heads], in_=rows[heads].rearrange("h (p t) c -> p h t c", t=PACK))
-            return raw
-
-        def regroup_head(copy, raw, grouped, h):
+        def regroup_head(copy, raw, grouped, h, g, first=0, last=DH):
             copy(
-                out=grouped[:, h].rearrange("p (c i) t -> p c t i", i=4),
-                in_=raw[:, h].rearrange("p t (c i) -> p c t i", i=4),
+                out=grouped[:, g, first:last].rearrange("p (c i) t -> p c t i", i=4),
+                in_=raw[:, h, :, first:last].rearrange("p t (c i) -> p c t i", i=4),
             )
 
-        def new_grouped(name):
-            return grouped_pool.tile([P, H, DH, PACK], BF16, name=name, tag="grouped", align_bytes=64)
+        def gpsimd_copy(out, in_):
+            nc.gpsimd.tensor_scalar(out=out, in0=in_, scalar1=1.0, scalar2=0.0, op0=MULT, op1=ADD)
 
         def new_quad_mx(name):
             codes = quad_mx.tile([P, H * DH], U32, name=name + "_codes", tag=name + "_codes", align_bytes=64)
@@ -88,18 +89,46 @@ def tile_mhla2_pa_t_kernel(tc, x_k, W_K, v_heads, out):
             return codes, scales
 
         def quantise_piece(grouped, codes, scales, piece):
-            heads = slice(piece * PIECE_HEADS, (piece + 1) * PIECE_HEADS)
             cols = slice(piece * PIECE_COLS, (piece + 1) * PIECE_COLS)
             nc.vector.quantize_mx(
                 out=codes[:, cols].bitcast(FP8X4),
                 scales=scales[:, cols],
-                in_=grouped[:, heads].rearrange("p h c t -> p (h c t)"),
+                in_=grouped[:].rearrange("p h c t -> p (h c t)"),
             )
 
-        def load_x(q):
+        w_raw = {}
+
+        def load_w(n, g):
+            heads = slice(n * HALF_HEADS, (n + 1) * HALF_HEADS)
+            w_raw[n, g] = w_pool.tile([P, HALF_HEADS, PACK, DH], BF16, name="w_raw", tag="w_raw")
+            rows = W_K[heads, g * K_PASS : (g + 1) * K_PASS, :]
+            nc.sync.dma_start(out=w_raw[n, g][:], in_=rows.rearrange("h (p t) c -> p h t c", t=PACK))
+
+        def regroup_w(n, g):
+            w_grouped[n, g] = w_pool.tile(
+                [P, HALF_HEADS, DH, PACK], BF16, name="w_grouped", tag="w_grouped", align_bytes=64
+            )
+            for h in range(HALF_HEADS):
+                copy = nc.scalar.copy if h == 3 else nc.vector.tensor_copy
+                regroup_head(copy, w_raw[n, g], w_grouped[n, g], h, h)
+
+        def quantise_w(n, g):
+            cols = slice(n * BANK, (n + 1) * BANK)
+            nc.vector.quantize_mx(
+                out=w_codes[:, g, cols].bitcast(FP8X4),
+                scales=w_scales[:, g, cols],
+                in_=w_grouped[n, g][:].rearrange("p h c t -> p (h c t)"),
+            )
+
+        def load_x(q, by_tile=False):
             b, rows = quad_rows(q)
             x_raw[q] = x_rows.tile([P, PACK, D], BF16, name="x_raw", tag="x_raw")
-            nc.sync.dma_start(out=x_raw[q][:], in_=x_k[b, rows, :].rearrange("(p j) d -> p j d", j=PACK))
+            source = x_k[b, rows, :].rearrange("(p j) d -> p j d", j=PACK)
+            if by_tile:
+                for j in range(PACK):
+                    nc.sync.dma_start(out=x_raw[q][:, j], in_=source[:, j])
+            else:
+                nc.sync.dma_start(out=x_raw[q][:], in_=source)
 
         def transpose_x(t):
             words = x_raw[t // PACK][:, t % PACK, :].bitcast(F32)
@@ -112,107 +141,149 @@ def tile_mhla2_pa_t_kernel(tc, x_k, W_K, v_heads, out):
                         words[:, g * pass_words + u : (g + 1) * pass_words : 2],
                         identity[:],
                     )
-            x_grouped[t] = x_grouped_pool.tile(
-                [P, FEATURE_PASSES * P * PACK], BF16, name="x_grouped", tag="x_grouped", align_bytes=64
-            )
+            turned_x[t] = turned
+
+        def copy_x(t):
+            pair, i = t // SLOT_TILES, t % SLOT_TILES
+            if i == 0:
+                x_grouped[pair] = x_grouped_pool.tile(
+                    [P, SLOT_TILES * D], BF16, name="x_grouped", tag="x_grouped", align_bytes=64
+                )
             nc.scalar.copy(
-                out=x_grouped[t][:].bitcast(F32).rearrange("p (g r u) -> p g r u", g=FEATURE_PASSES, u=2),
-                in_=turned[:].rearrange("p g u r -> p g r u"),
+                out=x_grouped[pair][:, i * D : (i + 1) * D].bitcast(F32).rearrange("p (g r u) -> p g r u", g=FEATURE_PASSES, u=2),
+                in_=turned_x[t][:].rearrange("p g u r -> p g r u"),
             )
 
-        def quantise_x(t):
-            x_codes[t] = x_mx.tile([P, FEATURE_PASSES * P], U32, name="x_codes", tag="x_codes", align_bytes=64)
-            x_scales[t] = x_mx.tile([P, FEATURE_PASSES * P], U8, name="x_scales", tag="x_scales", align_bytes=64)
+        def quantise_x(pair):
+            x_codes[pair] = x_mx.tile([P, SLOT_TILES * D // PACK], U32, name="x_codes", tag="x_codes", align_bytes=64)
+            x_scales[pair] = x_mx.tile([P, SLOT_TILES * D // PACK], U8, name="x_scales", tag="x_scales", align_bytes=64)
             nc.vector.quantize_mx(
-                out=x_codes[t][:].bitcast(FP8X4), scales=x_scales[t][:], in_=x_grouped[t][:]
+                out=x_codes[pair][:].bitcast(FP8X4), scales=x_scales[pair][:], in_=x_grouped[pair][:]
             )
 
-        def project(t):
-            k_banks[t] = []
-            for n in range(K_BANKS):
+        def slot_pair(s):
+            return (s // QUAD_SLOTS) * GROUP_SLOTS + s % GROUP_SLOTS
+
+        def project(s):
+            n = (s // GROUP_SLOTS) % HALVES
+            cols = slice(n * BANK, (n + 1) * BANK)
+            k_banks[s] = []
+            pair = slot_pair(s)
+            for i in range(SLOT_TILES):
                 bank = k_psum.tile([P, BANK], F32, name="k_bank", tag="k_bank")
                 for g in range(FEATURE_PASSES):
-                    tokens = slice(g * P, (g + 1) * P)
-                    cols = slice(n * BANK, (n + 1) * BANK)
+                    first = (i * FEATURE_PASSES + g) * P
+                    tokens = slice(first, first + P)
                     nc.tensor.matmul_mx(
                         out=bank[:],
-                        lhsT=x_codes[t][:, tokens].bitcast(FP8X4),
-                        lhsT_scale=x_scales[t][:, tokens],
+                        lhsT=x_codes[pair][:, tokens].bitcast(FP8X4),
+                        lhsT_scale=x_scales[pair][:, tokens],
                         rhs=w_codes[:, g, cols].bitcast(FP8X4),
                         rhs_scale=w_scales[:, g, cols],
                         start=(g == 0),
                         stop=(g == FEATURE_PASSES - 1),
                     )
-                k_banks[t].append(bank)
+                k_banks[s].append(bank)
 
-        def row_max(t):
-            largest = stats.tile([P, H], F32, name="largest", tag="largest")
-            for n in range(K_BANKS):
+        def row_max(s):
+            largest[s] = stats.tile([P, SLOT_TILES * HALF_HEADS], F32, name="largest", tag="largest")
+            for i in range(SLOT_TILES):
                 nc.vector.tensor_reduce(
-                    out=largest[:, n * HEADS_PER_BANK : (n + 1) * HEADS_PER_BANK],
-                    in_=k_banks[t][n][:].rearrange("p (h c) -> p h c", h=HEADS_PER_BANK),
+                    out=largest[s][:, i * HALF_HEADS : (i + 1) * HALF_HEADS],
+                    in_=k_banks[s][i][:].rearrange("p (h c) -> p h c", h=HALF_HEADS),
                     axis=AXIS_X,
                     op=MAX,
                 )
-            shift[t] = stats.tile([P, H], F32, name="shift", tag="shift")
-            nc.scalar.mul(out=shift[t][:], in_=largest[:], mul=-SOFTMAX_SCALE)
 
-        def exponentials(t):
-            q, j = t // PACK, t % PACK
-            if j == 0:
-                exps[q] = exp_pool.tile([P, PACK, H * DH], F32, name="exps", tag="exps")
-                sums[q] = stats.tile([P, H * PACK], F32, name="sums", tag="sums")
-            for h in range(H):
-                bank = k_banks[t][h // HEADS_PER_BANK]
-                first = (h % HEADS_PER_BANK) * DH
-                nc.scalar.activation(
-                    out=exps[q][:, j, h * DH : (h + 1) * DH],
-                    in_=bank[:, first : first + DH],
-                    func=EXP,
-                    bias=shift[t][:, h : h + 1],
-                    scale=SOFTMAX_SCALE,
-                    accum_out=sums[q][:, h * PACK + j : h * PACK + j + 1],
-                )
+        def shift_max(s):
+            shift[s] = stats.tile([P, SLOT_TILES * HALF_HEADS], F32, name="shift", tag="shift")
+            nc.scalar.mul(out=shift[s][:], in_=largest[s][:], mul=-SOFTMAX_SCALE)
 
-        def normalise(q, piece):
-            if piece == 0:
-                inv_sums[q] = stats.tile([P, H * PACK], F32, name="inv_sums", tag="inv_sums")
-                nc.vector.reciprocal(out=inv_sums[q][:], in_=sums[q][:])
-                p_grouped[q] = grouped_pool.tile(
-                    [P, H, DH, PACK], BF16, name="p_grouped", tag="p_grouped", align_bytes=64
-                )
-            for h in range(piece * PIECE_HEADS, (piece + 1) * PIECE_HEADS):
-                nc.vector.tensor_tensor(
-                    out=p_grouped[q][:, h].rearrange("p (c i) j -> p c j i", i=4),
-                    in0=exps[q][:, :, h * DH : (h + 1) * DH].rearrange("p j (c i) -> p c j i", i=4),
-                    in1=inv_sums[q][:, h * PACK : (h + 1) * PACK]
+        def exponentials(s):
+            group = s // GROUP_SLOTS
+            if s % GROUP_SLOTS == 0:
+                exps[group] = exp_pool.tile([P, PACK, BANK], F32, name="exps", tag="exps")
+                sums[group] = stats.tile([P, HALF_HEADS * PACK], F32, name="sums", tag="sums")
+            for i in range(SLOT_TILES):
+                j = (s % GROUP_SLOTS) * SLOT_TILES + i
+                for h in range(HALF_HEADS):
+                    nc.scalar.activation(
+                        out=exps[group][:, j, h * DH : (h + 1) * DH],
+                        in_=k_banks[s][i][:, h * DH : (h + 1) * DH],
+                        func=EXP,
+                        bias=shift[s][:, i * HALF_HEADS + h : i * HALF_HEADS + h + 1],
+                        scale=SOFTMAX_SCALE,
+                        accum_out=sums[group][:, h * PACK + j : h * PACK + j + 1],
+                    )
+
+        def invert(group):
+            inv_sums[group] = stats.tile([P, HALF_HEADS * PACK], F32, name="inv_sums", tag="inv_sums")
+            nc.vector.reciprocal(out=inv_sums[group][:], in_=sums[group][:])
+            inv_banks[group] = i_psum.tile([P, HALF_HEADS * PACK], F32, name="inv_bank", tag="inv_bank")
+            nc.tensor.matmul(
+                out=inv_banks[group][:], lhsT=identity[:], rhs=inv_sums[group][:], start=True, stop=True
+            )
+
+        def normalise(s):
+            group, piece = s // GROUP_SLOTS, s % GROUP_SLOTS
+            p_grouped[s] = grouped_pool.tile(
+                [P, PIECE_HEADS, DH, PACK], BF16, name="p_grouped", tag="p_grouped", align_bytes=64
+            )
+
+            def multiply(engine, inverse, i, first, last):
+                h = piece * PIECE_HEADS + i
+                engine.tensor_tensor(
+                    out=p_grouped[s][:, i, first:last].rearrange("p (c i) j -> p c j i", i=4),
+                    in0=exps[group][:, :, h * DH + first : h * DH + last].rearrange("p j (c i) -> p c j i", i=4),
+                    in1=inverse[:, h * PACK : (h + 1) * PACK]
                     .unsqueeze(1)
                     .unsqueeze(3)
-                    .to_broadcast([P, DH // 4, PACK, 4]),
+                    .to_broadcast([P, (last - first) // 4, PACK, 4]),
                     op=MULT,
                 )
 
-        def quantise_p(q, piece):
+            multiply(nc.vector, inv_banks[group], 0, 0, DH)
+            multiply(nc.gpsimd, inv_sums[group], 1, 0, DH)
+
+        def quantise_p(s):
+            q, piece = s // QUAD_SLOTS, s % QUAD_SLOTS
             if piece == 0:
                 p_codes[q], p_scales[q] = new_quad_mx("p")
-            quantise_piece(p_grouped[q], p_codes[q], p_scales[q], piece)
+            quantise_piece(p_grouped[s], p_codes[q], p_scales[q], piece)
 
         def load_v(q):
             b, rows = quad_rows(q)
-            v_raw[q] = load_k_first(v_heads[b, :, rows, :], "v_raw")
+            v_raw[q] = k_first_rows.tile([P, H, PACK, DH], BF16, name="v_raw", tag="v_raw")
+            for piece in range(QUAD_SLOTS):
+                heads = slice(piece * PIECE_HEADS, (piece + 1) * PIECE_HEADS)
+                nc.sync.dma_start(
+                    out=v_raw[q][:, heads], in_=v_heads[b, heads, rows, :].rearrange("h (p t) c -> p h t c", t=PACK)
+                )
 
-        def regroup_v(q, piece):
-            if piece == 0:
-                v_grouped[q] = new_grouped("v_grouped")
-            for h in range(piece * PIECE_HEADS, (piece + 1) * PIECE_HEADS):
-                regroup_head(nc.scalar.copy, v_raw[q], v_grouped[q], h)
+        def regroup_v(s):
+            q, piece, group = s // QUAD_SLOTS, s % QUAD_SLOTS, s // GROUP_SLOTS
+            if s % GROUP_SLOTS == 0:
+                v_grouped[group] = grouped_pool.tile(
+                    [P, HALF_HEADS, DH, PACK], BF16, name="v_grouped", tag="v_grouped", align_bytes=64
+                )
+            for i in range(PIECE_HEADS):
+                h = piece * PIECE_HEADS + i
+                g = h % HALF_HEADS
+                if i == 0:
+                    regroup_head(nc.scalar.copy, v_raw[q], v_grouped[group], h, g)
+                else:
+                    regroup_head(nc.scalar.copy, v_raw[q], v_grouped[group], h, g, 0, 64)
+                    regroup_head(nc.vector.tensor_copy, v_raw[q], v_grouped[group], h, g, 64, DH)
 
-        def quantise_v(q):
-            v_codes[q], v_scales[q] = new_quad_mx("v")
+        def quantise_v(group):
+            q, n = group // HALVES, group % HALVES
+            if n == 0:
+                v_codes[q], v_scales[q] = new_quad_mx("v")
+            cols = slice(n * BANK, (n + 1) * BANK)
             nc.vector.quantize_mx(
-                out=v_codes[q][:].bitcast(FP8X4),
-                scales=v_scales[q][:],
-                in_=v_grouped[q][:].rearrange("p h c t -> p (h c t)"),
+                out=v_codes[q][:, cols].bitcast(FP8X4),
+                scales=v_scales[q][:, cols],
+                in_=v_grouped[group][:].rearrange("p h c t -> p (h c t)"),
             )
 
         def summarise(b, piece):
@@ -236,9 +307,11 @@ def tile_mhla2_pa_t_kernel(tc, x_k, W_K, v_heads, out):
             heads = slice(piece * PIECE_HEADS, (piece + 1) * PIECE_HEADS)
             nc.sync.dma_start(out=out[b, heads].rearrange("h c e -> c h e"), in_=result[:])
 
-        w_raw = [load_k_first(W_K[:, 0:K_PASS, :], "w_raw")]
-        load_x(0)
-        w_raw.append(load_k_first(W_K[:, K_PASS : 2 * K_PASS, :], "w_raw"))
+        load_w(0, 0)
+        load_w(0, 1)
+        load_x(0, by_tile=True)
+        load_w(1, 0)
+        load_w(1, 1)
         load_v(0)
         load_x(1)
         load_v(1)
@@ -252,47 +325,53 @@ def tile_mhla2_pa_t_kernel(tc, x_k, W_K, v_heads, out):
 
         w_codes = keep.tile([P, FEATURE_PASSES, H * DH], U32, name="w_codes", align_bytes=64)
         w_scales = keep.tile([P, FEATURE_PASSES, H * DH], U8, name="w_scales", align_bytes=64)
-        w_grouped = []
         for g in range(FEATURE_PASSES):
-            w_grouped.append(new_grouped("w_grouped"))
-            for h in range(H):
-                copy = nc.scalar.copy if h % 3 == 2 else nc.vector.tensor_copy
-                regroup_head(copy, w_raw[g], w_grouped[g], h)
+            regroup_w(0, g)
         for g in range(FEATURE_PASSES):
-            nc.vector.quantize_mx(
-                out=w_codes[:, g, :].bitcast(FP8X4),
-                scales=w_scales[:, g, :],
-                in_=w_grouped[g][:].rearrange("p h c t -> p (h c t)"),
-            )
+            quantise_w(0, g)
 
         def in_stream(index):
-            return 0 <= index < TILES
+            return 0 <= index < SLOTS
 
-        for slot in range(-X_AHEAD, TILES + SUMMARY_BEHIND):
-            if slot >= 0 and slot % PACK == 0 and slot // PACK + LOAD_AHEAD < QUADS:
-                load_x(slot // PACK + LOAD_AHEAD)
-                load_v(slot // PACK + LOAD_AHEAD)
+        ctx.enter_context(tc.manual_schedule(engines={mybir.EngineType.DVE, mybir.EngineType.Pool}))
+        for slot in range(-X_AHEAD, SLOTS + SUMMARY_BEHIND):
+            if slot >= 0 and slot % QUAD_SLOTS == 0 and slot // QUAD_SLOTS + LOAD_AHEAD < QUADS:
+                load_x(slot // QUAD_SLOTS + LOAD_AHEAD)
+                load_v(slot // QUAD_SLOTS + LOAD_AHEAD)
 
-            if in_stream(slot + X_AHEAD):
-                transpose_x(slot + X_AHEAD)
             if in_stream(slot + 1):
                 project(slot + 1)
-            if in_stream(slot):
-                row_max(slot)
-            if in_stream(slot + V_AHEAD):
-                regroup_v((slot + V_AHEAD) // PACK, (slot + V_AHEAD) % PACK)
+            if in_stream(slot + X_AHEAD):
+                transpose_x(slot + X_AHEAD)
             if in_stream(slot):
                 exponentials(slot)
+            if in_stream(slot + X_AHEAD):
+                copy_x(slot + X_AHEAD)
+            if in_stream(slot - NORMALISE_BEHIND):
+                normalise(slot - NORMALISE_BEHIND)
+            if in_stream(slot + 1):
+                row_max(slot + 1)
+            if slot == -1:
+                for g in range(FEATURE_PASSES):
+                    regroup_w(1, g)
+                for g in range(FEATURE_PASSES):
+                    quantise_w(1, g)
+            if in_stream(slot + V_AHEAD):
+                regroup_v(slot + V_AHEAD)
+            if in_stream(slot + 1):
+                shift_max(slot + 1)
+            if in_stream(slot - 1) and (slot - 1) % GROUP_SLOTS == GROUP_SLOTS - 1:
+                invert((slot - 1) // GROUP_SLOTS)
 
             done = slot - SUMMARY_BEHIND
-            if in_stream(done) and (done // PACK) % QUADS_PER_BATCH == QUADS_PER_BATCH - 1:
-                summarise(done // PACK // QUADS_PER_BATCH, done % PACK)
+            if in_stream(done) and (done // QUAD_SLOTS) % QUADS_PER_BATCH == QUADS_PER_BATCH - 1:
+                summarise(done // QUAD_SLOTS // QUADS_PER_BATCH, done % QUAD_SLOTS)
 
-            if in_stream(slot - NORMALISE_BEHIND):
-                normalise((slot - NORMALISE_BEHIND) // PACK, (slot - NORMALISE_BEHIND) % PACK)
-            if in_stream(slot + X_AHEAD - 1):
-                quantise_x(slot + X_AHEAD - 1)
-            if in_stream(slot + V_AHEAD - 1) and (slot + V_AHEAD - 1) % PACK == PACK - 1:
-                quantise_v((slot + V_AHEAD - 1) // PACK)
+            x_tile = slot + X_AHEAD - 1
+            if in_stream(x_tile) and x_tile % SLOT_TILES == SLOT_TILES - 1:
+                quantise_x(x_tile // SLOT_TILES)
+            v_piece = slot + V_AHEAD - 1
+            if in_stream(v_piece) and v_piece % GROUP_SLOTS == GROUP_SLOTS - 1:
+                quantise_v(v_piece // GROUP_SLOTS)
             if in_stream(slot - QUANTISE_P_BEHIND):
-                quantise_p((slot - QUANTISE_P_BEHIND) // PACK, (slot - QUANTISE_P_BEHIND) % PACK)
+                quantise_p(slot - QUANTISE_P_BEHIND)

@@ -230,20 +230,23 @@ def tile_mhla2_pa_t_kernel(tc, x_k, W_K, v_heads, out):
                 [P, PIECE_HEADS, DH, PACK], BF16, name="p_grouped", tag="p_grouped", align_bytes=64
             )
 
-            def multiply(engine, inverse, i, first, last):
-                h = piece * PIECE_HEADS + i
-                engine.tensor_tensor(
-                    out=p_grouped[s][:, i, first:last].rearrange("p (c i) j -> p c j i", i=4),
-                    in0=exps[group][:, :, h * DH + first : h * DH + last].rearrange("p j (c i) -> p c j i", i=4),
-                    in1=inverse[:, h * PACK : (h + 1) * PACK]
-                    .unsqueeze(1)
-                    .unsqueeze(3)
-                    .to_broadcast([P, (last - first) // 4, PACK, 4]),
-                    op=MULT,
-                )
-
-            multiply(nc.vector, inv_banks[group], 0, 0, DH)
-            multiply(nc.gpsimd, inv_sums[group], 1, 0, DH)
+            h = piece * PIECE_HEADS
+            nc.vector.tensor_tensor(
+                out=p_grouped[s][:, 0].rearrange("p (c i) j -> p c j i", i=4),
+                in0=exps[group][:, :, h * DH : (h + 1) * DH].rearrange("p j (c i) -> p c j i", i=4),
+                in1=inv_banks[group][:, h * PACK : (h + 1) * PACK]
+                .unsqueeze(1)
+                .unsqueeze(3)
+                .to_broadcast([P, DH // 4, PACK, 4]),
+                op=MULT,
+            )
+            h += 1
+            nc.gpsimd.tensor_tensor(
+                out=p_grouped[s][:, 1],
+                in0=exps[group][:, :, h * DH : (h + 1) * DH].rearrange("p j c -> p c j"),
+                in1=inv_sums[group][:, h * PACK : (h + 1) * PACK].unsqueeze(1).to_broadcast([P, DH, PACK]),
+                op=MULT,
+            )
 
         def quantise_p(s):
             q, piece = s // QUAD_SLOTS, s % QUAD_SLOTS

@@ -37,11 +37,10 @@ PIECE_COLS = PIECE_HEADS * DH
 SOFTMAX_SCALE = 1.0 / DH**0.25
 
 X_AHEAD = 6
-V_AHEAD = 1
-NORMALISE_BEHIND = GROUP_SLOTS + 1
+NORMALISE_BEHIND = GROUP_SLOTS
 QUANTISE_P_BEHIND = NORMALISE_BEHIND + 1
-SUMMARY_BEHIND = QUANTISE_P_BEHIND + 1
-LOAD_AHEAD = 2
+X_LOAD_AHEAD = 3
+V_LOAD_AHEAD = 2
 
 FLOPS = 2 * B * S * D * H * DH + 2 * B * H * S * DH * DH
 
@@ -51,18 +50,20 @@ def tile_mhla2_pa_t_kernel(tc, x_k, W_K, v_heads, out):
     with ExitStack() as ctx:
         keep = ctx.enter_context(tc.tile_pool(name="keep", bufs=1))
         x_rows = ctx.enter_context(tc.tile_pool(name="x_rows", bufs=4))
-        k_first_rows = ctx.enter_context(tc.tile_pool(name="k_first_rows", bufs=3))
-        w_pool = ctx.enter_context(tc.tile_pool(name="w_pool", bufs=4))
+        v_rows = ctx.enter_context(tc.tile_pool(name="v_rows", bufs=4))
+        w_rows = ctx.enter_context(tc.tile_pool(name="w_rows", bufs=4))
+        w_grouped_pool = ctx.enter_context(tc.tile_pool(name="w_grouped", bufs=2))
+        v_grouped_pool = ctx.enter_context(tc.tile_pool(name="v_grouped", bufs=4))
         grouped_pool = ctx.enter_context(tc.tile_pool(name="grouped", bufs=2))
-        x_grouped_pool = ctx.enter_context(tc.tile_pool(name="x_grouped", bufs=2))
-        x_mx = ctx.enter_context(tc.tile_pool(name="x_mx", bufs=5))
+        x_grouped_pool = ctx.enter_context(tc.tile_pool(name="x_grouped", bufs=3))
+        x_mx = ctx.enter_context(tc.tile_pool(name="x_mx", bufs=6))
         quad_mx = ctx.enter_context(tc.tile_pool(name="quad_mx", bufs=QUADS_PER_BATCH + 2))
         exp_pool = ctx.enter_context(tc.tile_pool(name="exp", bufs=3))
         stats = ctx.enter_context(tc.tile_pool(name="stats", bufs=4))
         result_pool = ctx.enter_context(tc.tile_pool(name="result", bufs=4))
         k_psum = ctx.enter_context(tc.psum_pool(name="k_psum", bufs=4))
-        t_psum = ctx.enter_context(tc.psum_pool(name="t_psum", bufs=2))
         o_psum = ctx.enter_context(tc.psum_pool(name="o_psum", bufs=1))
+        t_psum = ctx.enter_context(tc.psum_pool(name="t_psum", bufs=2))
         i_psum = ctx.enter_context(tc.psum_pool(name="i_psum", bufs=1))
 
         x_raw, turned_x, v_raw, v_grouped, v_codes, v_scales = {}, {}, {}, {}, {}, {}
@@ -100,16 +101,16 @@ def tile_mhla2_pa_t_kernel(tc, x_k, W_K, v_heads, out):
 
         def load_w(n, g):
             heads = slice(n * HALF_HEADS, (n + 1) * HALF_HEADS)
-            w_raw[n, g] = w_pool.tile([P, HALF_HEADS, PACK, DH], BF16, name="w_raw", tag="w_raw")
+            w_raw[n, g] = w_rows.tile([P, HALF_HEADS, PACK, DH], BF16, name="w_raw", tag="w_raw")
             rows = W_K[heads, g * K_PASS : (g + 1) * K_PASS, :]
             nc.sync.dma_start(out=w_raw[n, g][:], in_=rows.rearrange("h (p t) c -> p h t c", t=PACK))
 
-        def regroup_w(n, g):
-            w_grouped[n, g] = w_pool.tile(
-                [P, HALF_HEADS, DH, PACK], BF16, name="w_grouped", tag="w_grouped", align_bytes=64
-            )
-            for h in range(HALF_HEADS):
-                copy = nc.scalar.copy if h == 3 else nc.vector.tensor_copy
+        def regroup_w(n, g, heads, copy):
+            if heads[0] == 0:
+                w_grouped[n, g] = w_grouped_pool.tile(
+                    [P, HALF_HEADS, DH, PACK], BF16, name="w_grouped", tag="w_grouped", align_bytes=64
+                )
+            for h in heads:
                 regroup_head(copy, w_raw[n, g], w_grouped[n, g], h, h)
 
         def quantise_w(n, g):
@@ -120,15 +121,13 @@ def tile_mhla2_pa_t_kernel(tc, x_k, W_K, v_heads, out):
                 in_=w_grouped[n, g][:].rearrange("p h c t -> p (h c t)"),
             )
 
-        def load_x(q, by_tile=False):
+        def load_x(q, first, last, tiles=1):
             b, rows = quad_rows(q)
-            x_raw[q] = x_rows.tile([P, PACK, D], BF16, name="x_raw", tag="x_raw")
+            if first == 0:
+                x_raw[q] = x_rows.tile([P, PACK, D], BF16, name="x_raw", tag="x_raw")
             source = x_k[b, rows, :].rearrange("(p j) d -> p j d", j=PACK)
-            if by_tile:
-                for j in range(PACK):
-                    nc.sync.dma_start(out=x_raw[q][:, j], in_=source[:, j])
-            else:
-                nc.sync.dma_start(out=x_raw[q][:], in_=source)
+            for j in range(first, last, tiles):
+                nc.sync.dma_start(out=x_raw[q][:, j : j + tiles], in_=source[:, j : j + tiles])
 
         def transpose_x(t):
             words = x_raw[t // PACK][:, t % PACK, :].bitcast(F32)
@@ -164,61 +163,60 @@ def tile_mhla2_pa_t_kernel(tc, x_k, W_K, v_heads, out):
         def slot_pair(s):
             return (s // QUAD_SLOTS) * GROUP_SLOTS + s % GROUP_SLOTS
 
-        def project(s):
+        def project(s, i):
             n = (s // GROUP_SLOTS) % HALVES
             cols = slice(n * BANK, (n + 1) * BANK)
-            k_banks[s] = []
             pair = slot_pair(s)
-            for i in range(SLOT_TILES):
-                bank = k_psum.tile([P, BANK], F32, name="k_bank", tag="k_bank")
-                for g in range(FEATURE_PASSES):
-                    first = (i * FEATURE_PASSES + g) * P
-                    tokens = slice(first, first + P)
-                    nc.tensor.matmul_mx(
-                        out=bank[:],
-                        lhsT=x_codes[pair][:, tokens].bitcast(FP8X4),
-                        lhsT_scale=x_scales[pair][:, tokens],
-                        rhs=w_codes[:, g, cols].bitcast(FP8X4),
-                        rhs_scale=w_scales[:, g, cols],
-                        start=(g == 0),
-                        stop=(g == FEATURE_PASSES - 1),
-                    )
-                k_banks[s].append(bank)
-
-        def row_max(s):
-            largest[s] = stats.tile([P, SLOT_TILES * HALF_HEADS], F32, name="largest", tag="largest")
-            for i in range(SLOT_TILES):
-                nc.vector.tensor_reduce(
-                    out=largest[s][:, i * HALF_HEADS : (i + 1) * HALF_HEADS],
-                    in_=k_banks[s][i][:].rearrange("p (h c) -> p h c", h=HALF_HEADS),
-                    axis=AXIS_X,
-                    op=MAX,
+            bank = k_psum.tile([P, BANK], F32, name="k_bank", tag="k_bank")
+            for g in range(FEATURE_PASSES):
+                first = (i * FEATURE_PASSES + g) * P
+                tokens = slice(first, first + P)
+                nc.tensor.matmul_mx(
+                    out=bank[:],
+                    lhsT=x_codes[pair][:, tokens].bitcast(FP8X4),
+                    lhsT_scale=x_scales[pair][:, tokens],
+                    rhs=w_codes[:, g, cols].bitcast(FP8X4),
+                    rhs_scale=w_scales[:, g, cols],
+                    start=(g == 0),
+                    stop=(g == FEATURE_PASSES - 1),
                 )
+            k_banks[s, i] = bank
+
+        def row_max(s, i):
+            if i == 0:
+                largest[s] = stats.tile([P, SLOT_TILES * HALF_HEADS], F32, name="largest", tag="largest")
+            nc.vector.tensor_reduce(
+                out=largest[s][:, i * HALF_HEADS : (i + 1) * HALF_HEADS],
+                in_=k_banks[s, i][:].rearrange("p (h c) -> p h c", h=HALF_HEADS),
+                axis=AXIS_X,
+                op=MAX,
+            )
 
         def shift_max(s):
             shift[s] = stats.tile([P, SLOT_TILES * HALF_HEADS], F32, name="shift", tag="shift")
             nc.scalar.mul(out=shift[s][:], in_=largest[s][:], mul=-SOFTMAX_SCALE)
 
-        def exponentials(s):
+        def exponentials(s, i):
             group = s // GROUP_SLOTS
-            if s % GROUP_SLOTS == 0:
+            j = (s % GROUP_SLOTS) * SLOT_TILES + i
+            if j == 0:
                 exps[group] = exp_pool.tile([P, PACK, BANK], F32, name="exps", tag="exps")
                 sums[group] = stats.tile([P, HALF_HEADS * PACK], F32, name="sums", tag="sums")
-            for i in range(SLOT_TILES):
-                j = (s % GROUP_SLOTS) * SLOT_TILES + i
-                for h in range(HALF_HEADS):
-                    nc.scalar.activation(
-                        out=exps[group][:, j, h * DH : (h + 1) * DH],
-                        in_=k_banks[s][i][:, h * DH : (h + 1) * DH],
-                        func=EXP,
-                        bias=shift[s][:, i * HALF_HEADS + h : i * HALF_HEADS + h + 1],
-                        scale=SOFTMAX_SCALE,
-                        accum_out=sums[group][:, h * PACK + j : h * PACK + j + 1],
-                    )
+            for h in range(HALF_HEADS):
+                nc.scalar.activation(
+                    out=exps[group][:, j, h * DH : (h + 1) * DH],
+                    in_=k_banks[s, i][:, h * DH : (h + 1) * DH],
+                    func=EXP,
+                    bias=shift[s][:, i * HALF_HEADS + h : i * HALF_HEADS + h + 1],
+                    scale=SOFTMAX_SCALE,
+                    accum_out=sums[group][:, h * PACK + j : h * PACK + j + 1],
+                )
 
         def invert(group):
             inv_sums[group] = stats.tile([P, HALF_HEADS * PACK], F32, name="inv_sums", tag="inv_sums")
             nc.vector.reciprocal(out=inv_sums[group][:], in_=sums[group][:])
+
+        def spread_inverse(group):
             inv_banks[group] = i_psum.tile([P, HALF_HEADS * PACK], F32, name="inv_bank", tag="inv_bank")
             nc.tensor.matmul(
                 out=inv_banks[group][:], lhsT=identity[:], rhs=inv_sums[group][:], start=True, stop=True
@@ -230,23 +228,23 @@ def tile_mhla2_pa_t_kernel(tc, x_k, W_K, v_heads, out):
                 [P, PIECE_HEADS, DH, PACK], BF16, name="p_grouped", tag="p_grouped", align_bytes=64
             )
 
-            h = piece * PIECE_HEADS
-            nc.vector.tensor_tensor(
-                out=p_grouped[s][:, 0].rearrange("p (c i) j -> p c j i", i=4),
-                in0=exps[group][:, :, h * DH : (h + 1) * DH].rearrange("p j (c i) -> p c j i", i=4),
-                in1=inv_banks[group][:, h * PACK : (h + 1) * PACK]
-                .unsqueeze(1)
-                .unsqueeze(3)
-                .to_broadcast([P, DH // 4, PACK, 4]),
-                op=MULT,
-            )
-            h += 1
-            nc.gpsimd.tensor_tensor(
-                out=p_grouped[s][:, 1],
-                in0=exps[group][:, :, h * DH : (h + 1) * DH].rearrange("p j c -> p c j"),
-                in1=inv_sums[group][:, h * PACK : (h + 1) * PACK].unsqueeze(1).to_broadcast([P, DH, PACK]),
-                op=MULT,
-            )
+            def multiply(engine, inverse, i, first, last):
+                h = piece * PIECE_HEADS + i
+                engine.tensor_tensor(
+                    out=p_grouped[s][:, i, first:last].rearrange("p (c i) j -> p c j i", i=4),
+                    in0=exps[group][:, :, h * DH + first : h * DH + last].rearrange("p j (c i) -> p c j i", i=4),
+                    in1=inverse[:, h * PACK : (h + 1) * PACK]
+                    .unsqueeze(1)
+                    .unsqueeze(3)
+                    .to_broadcast([P, (last - first) // 4, PACK, 4]),
+                    op=MULT,
+                )
+
+            multiply(nc.vector, inv_banks[group], 0, 0, DH)
+            if s == SLOTS - 2:
+                multiply(nc.vector, inv_banks[group], 1, 0, DH)
+            else:
+                multiply(nc.gpsimd, inv_sums[group], 1, 0, DH)
 
         def quantise_p(s):
             q, piece = s // QUAD_SLOTS, s % QUAD_SLOTS
@@ -256,7 +254,7 @@ def tile_mhla2_pa_t_kernel(tc, x_k, W_K, v_heads, out):
 
         def load_v(q):
             b, rows = quad_rows(q)
-            v_raw[q] = k_first_rows.tile([P, H, PACK, DH], BF16, name="v_raw", tag="v_raw")
+            v_raw[q] = v_rows.tile([P, H, PACK, DH], BF16, name="v_raw", tag="v_raw")
             for piece in range(QUAD_SLOTS):
                 heads = slice(piece * PIECE_HEADS, (piece + 1) * PIECE_HEADS)
                 nc.sync.dma_start(
@@ -266,17 +264,13 @@ def tile_mhla2_pa_t_kernel(tc, x_k, W_K, v_heads, out):
         def regroup_v(s):
             q, piece, group = s // QUAD_SLOTS, s % QUAD_SLOTS, s // GROUP_SLOTS
             if s % GROUP_SLOTS == 0:
-                v_grouped[group] = grouped_pool.tile(
+                v_grouped[group] = v_grouped_pool.tile(
                     [P, HALF_HEADS, DH, PACK], BF16, name="v_grouped", tag="v_grouped", align_bytes=64
                 )
             for i in range(PIECE_HEADS):
                 h = piece * PIECE_HEADS + i
-                g = h % HALF_HEADS
-                if i == 0:
-                    regroup_head(nc.scalar.copy, v_raw[q], v_grouped[group], h, g)
-                else:
-                    regroup_head(nc.scalar.copy, v_raw[q], v_grouped[group], h, g, 0, 64)
-                    regroup_head(nc.vector.tensor_copy, v_raw[q], v_grouped[group], h, g, 64, DH)
+                copy = nc.scalar.copy if i == 0 else nc.vector.tensor_copy
+                regroup_head(copy, v_raw[q], v_grouped[group], h, h % HALF_HEADS)
 
         def quantise_v(group):
             q, n = group // HALVES, group % HALVES
@@ -289,7 +283,8 @@ def tile_mhla2_pa_t_kernel(tc, x_k, W_K, v_heads, out):
                 in_=v_grouped[group][:].rearrange("p h c t -> p (h c t)"),
             )
 
-        def summarise(b, piece):
+        def summarise(s):
+            b, piece = s // QUAD_SLOTS // QUADS_PER_BATCH, s % QUAD_SLOTS
             summary = o_psum.tile([P, PIECE_HEADS, DH], F32, name="summary", tag="summary")
             for i in range(PIECE_HEADS):
                 h = piece * PIECE_HEADS + i
@@ -310,13 +305,15 @@ def tile_mhla2_pa_t_kernel(tc, x_k, W_K, v_heads, out):
             heads = slice(piece * PIECE_HEADS, (piece + 1) * PIECE_HEADS)
             nc.sync.dma_start(out=out[b, heads].rearrange("h c e -> c h e"), in_=result[:])
 
+        load_x(0, 0, 2)
         load_w(0, 0)
         load_w(0, 1)
-        load_x(0, by_tile=True)
+        load_x(0, 2, 4)
         load_w(1, 0)
         load_w(1, 1)
+        load_x(1, 0, 4)
         load_v(0)
-        load_x(1)
+        load_x(2, 0, 4, PACK)
         load_v(1)
 
         identity = keep.tile([P, P], F32, name="identity")
@@ -328,53 +325,112 @@ def tile_mhla2_pa_t_kernel(tc, x_k, W_K, v_heads, out):
 
         w_codes = keep.tile([P, FEATURE_PASSES, H * DH], U32, name="w_codes", align_bytes=64)
         w_scales = keep.tile([P, FEATURE_PASSES, H * DH], U8, name="w_scales", align_bytes=64)
-        for g in range(FEATURE_PASSES):
-            regroup_w(0, g)
-        for g in range(FEATURE_PASSES):
-            quantise_w(0, g)
 
-        def in_stream(index):
-            return 0 <= index < SLOTS
+        ctx.enter_context(tc.manual_schedule())
+        V_HEADS, S_HEADS = (0, 1, 2), (3,)
 
-        ctx.enter_context(tc.manual_schedule(engines={mybir.EngineType.DVE, mybir.EngineType.Pool}))
-        for slot in range(-X_AHEAD, SLOTS + SUMMARY_BEHIND):
-            if slot >= 0 and slot % QUAD_SLOTS == 0 and slot // QUAD_SLOTS + LOAD_AHEAD < QUADS:
-                load_x(slot // QUAD_SLOTS + LOAD_AHEAD)
-                load_v(slot // QUAD_SLOTS + LOAD_AHEAD)
+        def regroup_w_shared(n, g):
+            regroup_w(n, g, V_HEADS, nc.vector.tensor_copy)
+            regroup_w(n, g, S_HEADS, nc.scalar.copy)
 
-            if in_stream(slot + 1):
-                project(slot + 1)
-            if in_stream(slot + X_AHEAD):
-                transpose_x(slot + X_AHEAD)
-            if in_stream(slot):
-                exponentials(slot)
-            if in_stream(slot + X_AHEAD):
-                copy_x(slot + X_AHEAD)
-            if in_stream(slot - NORMALISE_BEHIND):
+        transpose_x(0)
+        transpose_x(1)
+        copy_x(0)
+        regroup_w_shared(0, 0)
+        quantise_w(0, 0)
+        copy_x(1)
+        regroup_w_shared(0, 1)
+        quantise_x(0)
+        quantise_w(0, 1)
+        transpose_x(2)
+        transpose_x(3)
+        copy_x(2)
+        copy_x(3)
+        for i in range(SLOT_TILES):
+            project(0, i)
+        regroup_w(1, 0, (0, 1, 2), nc.vector.tensor_copy)
+        quantise_x(1)
+        for i in range(SLOT_TILES):
+            row_max(0, i)
+        regroup_w(1, 0, (3,), nc.scalar.copy)
+        regroup_w(1, 1, (0, 1), nc.scalar.copy)
+        shift_max(0)
+        for i in range(SLOT_TILES):
+            project(1, i)
+        transpose_x(4)
+        transpose_x(5)
+
+        LAST = SLOTS - 1
+
+        def turn_slot(t):
+            return max(t - X_AHEAD, -1)
+
+        def regroup_v_slot(s):
+            return s + 1 - s // 8
+
+        v_slots = [s for s in range(SLOTS) if s % QUAD_SLOTS in (0, 3) or s >= SLOTS - QUAD_SLOTS]
+        v_slots = v_slots[-GROUPS:]
+
+        for slot in range(SLOTS + 1):
+            q, phase = slot // QUAD_SLOTS, slot % QUAD_SLOTS
+            if phase == 0 and q + X_LOAD_AHEAD < QUADS:
+                load_x(q + X_LOAD_AHEAD, 0, 4, PACK)
+            if phase == 0 and q + V_LOAD_AHEAD < QUADS:
+                load_v(q + V_LOAD_AHEAD)
+
+            closed = (slot - 1) // GROUP_SLOTS if slot > 0 and phase % GROUP_SLOTS == 0 else None
+            if slot == SLOTS:
+                quantise_p(slot - QUANTISE_P_BEHIND)
+            if closed is not None:
+                invert(closed)
+
+            if 0 < slot < LAST:
+                project(slot + 1, 0)
+            if slot < SLOTS:
+                exponentials(slot, 0)
+            for t in range(PACK, TILES):
+                if turn_slot(t) == slot - 1:
+                    copy_x(t)
+            for t in range(PACK, TILES):
+                if turn_slot(t) == slot:
+                    transpose_x(t)
+            if 0 < slot < LAST:
+                project(slot + 1, 1)
+            if closed is not None:
+                spread_inverse(closed)
+            if slot < SLOTS:
+                exponentials(slot, 1)
+
+            if slot < LAST:
+                row_max(slot + 1, 0)
+            if closed is None and slot >= NORMALISE_BEHIND:
                 normalise(slot - NORMALISE_BEHIND)
-            if in_stream(slot + 1):
-                row_max(slot + 1)
-            if slot == -1:
-                for g in range(FEATURE_PASSES):
-                    regroup_w(1, g)
+            if slot < LAST:
+                row_max(slot + 1, 1)
+            if closed is not None and slot >= NORMALISE_BEHIND:
+                normalise(slot - NORMALISE_BEHIND)
+            if slot == SLOTS:
+                normalise(LAST)
+            if slot < LAST:
+                shift_max(slot + 1)
+            for s in range(SLOTS):
+                if regroup_v_slot(s) == slot:
+                    regroup_v(s)
+            if slot == 0:
+                regroup_w(1, 1, (2, 3), nc.vector.tensor_copy)
                 for g in range(FEATURE_PASSES):
                     quantise_w(1, g)
-            if in_stream(slot + V_AHEAD):
-                regroup_v(slot + V_AHEAD)
-            if in_stream(slot + 1):
-                shift_max(slot + 1)
-            if in_stream(slot - 1) and (slot - 1) % GROUP_SLOTS == GROUP_SLOTS - 1:
-                invert((slot - 1) // GROUP_SLOTS)
 
-            done = slot - SUMMARY_BEHIND
-            if in_stream(done) and (done // QUAD_SLOTS) % QUADS_PER_BATCH == QUADS_PER_BATCH - 1:
-                summarise(done // QUAD_SLOTS // QUADS_PER_BATCH, done % QUAD_SLOTS)
-
-            x_tile = slot + X_AHEAD - 1
-            if in_stream(x_tile) and x_tile % SLOT_TILES == SLOT_TILES - 1:
-                quantise_x(x_tile // SLOT_TILES)
-            v_piece = slot + V_AHEAD - 1
-            if in_stream(v_piece) and v_piece % GROUP_SLOTS == GROUP_SLOTS - 1:
-                quantise_v(v_piece // GROUP_SLOTS)
-            if in_stream(slot - QUANTISE_P_BEHIND):
+            if slot in v_slots:
+                quantise_v(v_slots.index(slot))
+            if phase in (1, 2) and q < QUADS - 1:
+                quantise_x((q + 1) * GROUP_SLOTS + phase - 1)
+            if QUANTISE_P_BEHIND <= slot < SLOTS:
                 quantise_p(slot - QUANTISE_P_BEHIND)
+            if slot == SLOTS:
+                quantise_p(LAST - 1)
+                quantise_p(LAST)
+            for s in range(SLOTS):
+                summary_slot = min(s + QUANTISE_P_BEHIND + 4, SLOTS)
+                if summary_slot == slot and (s // QUAD_SLOTS) % QUADS_PER_BATCH == QUADS_PER_BATCH - 1:
+                    summarise(s)

@@ -69,7 +69,7 @@ def tile_mhla2_pa_t_kernel(tc, x_k, W_K, v_heads, out):
         x_raw, turned_x, v_raw, v_grouped, v_codes, v_scales = {}, {}, {}, {}, {}, {}
         x_grouped, x_codes, x_scales, k_banks, largest, shift = {}, {}, {}, {}, {}, {}
         exps, sums, inv_sums, inv_banks, p_grouped, p_codes, p_scales = {}, {}, {}, {}, {}, {}, {}
-        w_grouped = {}
+        w_grouped, last_banks = {}, {}
 
         def quad_rows(q):
             first = (q % QUADS_PER_BATCH) * K_PASS
@@ -240,11 +240,12 @@ def tile_mhla2_pa_t_kernel(tc, x_k, W_K, v_heads, out):
                     op=MULT,
                 )
 
-            multiply(nc.vector, inv_banks[group], 0, 0, DH)
-            if s == SLOTS - 2:
+            if s in (SLOTS - 3, SLOTS - 2):
+                multiply(nc.vector, inv_banks[group], 0, 0, DH)
                 multiply(nc.vector, inv_banks[group], 1, 0, DH)
             else:
                 multiply(nc.gpsimd, inv_sums[group], 1, 0, DH)
+                multiply(nc.vector, inv_banks[group], 0, 0, DH)
 
         def quantise_p(s):
             q, piece = s // QUAD_SLOTS, s % QUAD_SLOTS
@@ -269,8 +270,12 @@ def tile_mhla2_pa_t_kernel(tc, x_k, W_K, v_heads, out):
                 )
             for i in range(PIECE_HEADS):
                 h = piece * PIECE_HEADS + i
-                copy = nc.scalar.copy if i == 0 else nc.vector.tensor_copy
-                regroup_head(copy, v_raw[q], v_grouped[group], h, h % HALF_HEADS)
+                g = h % HALF_HEADS
+                split = DH if i == 0 or s >= 28 else 32
+                if split > 0:
+                    regroup_head(nc.scalar.copy, v_raw[q], v_grouped[group], h, g, 0, split)
+                if split < DH:
+                    regroup_head(nc.vector.tensor_copy, v_raw[q], v_grouped[group], h, g, split, DH)
 
         def quantise_v(group):
             q, n = group // HALVES, group % HALVES
@@ -283,27 +288,45 @@ def tile_mhla2_pa_t_kernel(tc, x_k, W_K, v_heads, out):
                 in_=v_grouped[group][:].rearrange("p h c t -> p (h c t)"),
             )
 
-        def summarise(s):
-            b, piece = s // QUAD_SLOTS // QUADS_PER_BATCH, s % QUAD_SLOTS
-            summary = o_psum.tile([P, PIECE_HEADS, DH], F32, name="summary", tag="summary")
-            for i in range(PIECE_HEADS):
-                h = piece * PIECE_HEADS + i
-                cols = slice(h * DH, (h + 1) * DH)
-                for n in range(QUADS_PER_BATCH):
-                    q = b * QUADS_PER_BATCH + n
-                    nc.tensor.matmul_mx(
-                        out=summary[:, i, :],
-                        lhsT=p_codes[q][:, cols].bitcast(FP8X4),
-                        lhsT_scale=p_scales[q][:, cols],
-                        rhs=v_codes[q][:, cols].bitcast(FP8X4),
-                        rhs_scale=v_scales[q][:, cols],
-                        start=(n == 0),
-                        stop=(n == QUADS_PER_BATCH - 1),
-                    )
-            result = result_pool.tile([P, PIECE_HEADS, DH], F32, name="result", tag="result")
-            nc.scalar.copy(out=result[:], in_=summary[:])
+        def add_quads(b, h, quads, bank):
+            cols = slice(h * DH, (h + 1) * DH)
+            for n in quads:
+                q = b * QUADS_PER_BATCH + n
+                nc.tensor.matmul_mx(
+                    out=bank,
+                    lhsT=p_codes[q][:, cols].bitcast(FP8X4),
+                    lhsT_scale=p_scales[q][:, cols],
+                    rhs=v_codes[q][:, cols].bitcast(FP8X4),
+                    rhs_scale=v_scales[q][:, cols],
+                    start=(n == 0),
+                    stop=(n == QUADS_PER_BATCH - 1),
+                )
+
+        def store(b, piece, result):
             heads = slice(piece * PIECE_HEADS, (piece + 1) * PIECE_HEADS)
             nc.sync.dma_start(out=out[b, heads].rearrange("h c e -> c h e"), in_=result[:])
+
+        def summarise(s, pool, tag):
+            b, piece = s // QUAD_SLOTS // QUADS_PER_BATCH, s % QUAD_SLOTS
+            summary = pool.tile([P, PIECE_HEADS, DH], F32, name="summary", tag=tag)
+            for i in range(PIECE_HEADS):
+                add_quads(b, piece * PIECE_HEADS + i, range(QUADS_PER_BATCH), summary[:, i])
+            result = result_pool.tile([P, PIECE_HEADS, DH], F32, name="result", tag="result")
+            nc.scalar.copy(out=result[:], in_=summary[:])
+            store(b, piece, result)
+
+        def open_summary(h, pool, tag):
+            last_banks[h] = pool.tile([P, DH], F32, name="last_bank", tag=tag)
+            add_quads(B - 1, h, range(QUADS_PER_BATCH - 1), last_banks[h][:])
+
+        def close_summaries(piece):
+            result = result_pool.tile([P, PIECE_HEADS, DH], F32, name="result", tag="result")
+            for i in range(PIECE_HEADS):
+                h = piece * PIECE_HEADS + i
+                add_quads(B - 1, h, (QUADS_PER_BATCH - 1,), last_banks[h][:])
+                copy = nc.scalar.copy if i == 0 else nc.vector.tensor_copy
+                copy(out=result[:, i], in_=last_banks[h][:])
+            store(B - 1, piece, result)
 
         load_x(0, 0, 2)
         load_w(0, 0)
@@ -371,7 +394,7 @@ def tile_mhla2_pa_t_kernel(tc, x_k, W_K, v_heads, out):
         v_slots = [s for s in range(SLOTS) if s % QUAD_SLOTS in (0, 3) or s >= SLOTS - QUAD_SLOTS]
         v_slots = v_slots[-GROUPS:]
 
-        for slot in range(SLOTS + 1):
+        for slot in range(SLOTS):
             q, phase = slot // QUAD_SLOTS, slot % QUAD_SLOTS
             if phase == 0 and q + X_LOAD_AHEAD < QUADS:
                 load_x(q + X_LOAD_AHEAD, 0, 4, PACK)
@@ -379,15 +402,12 @@ def tile_mhla2_pa_t_kernel(tc, x_k, W_K, v_heads, out):
                 load_v(q + V_LOAD_AHEAD)
 
             closed = (slot - 1) // GROUP_SLOTS if slot > 0 and phase % GROUP_SLOTS == 0 else None
-            if slot == SLOTS:
-                quantise_p(slot - QUANTISE_P_BEHIND)
             if closed is not None:
                 invert(closed)
 
             if 0 < slot < LAST:
                 project(slot + 1, 0)
-            if slot < SLOTS:
-                exponentials(slot, 0)
+            exponentials(slot, 0)
             for t in range(PACK, TILES):
                 if turn_slot(t) == slot - 1:
                     copy_x(t)
@@ -398,19 +418,16 @@ def tile_mhla2_pa_t_kernel(tc, x_k, W_K, v_heads, out):
                 project(slot + 1, 1)
             if closed is not None:
                 spread_inverse(closed)
-            if slot < SLOTS:
-                exponentials(slot, 1)
+            exponentials(slot, 1)
 
             if slot < LAST:
                 row_max(slot + 1, 0)
-            if closed is None and slot >= NORMALISE_BEHIND:
+            if closed is None and NORMALISE_BEHIND <= slot < LAST:
                 normalise(slot - NORMALISE_BEHIND)
             if slot < LAST:
                 row_max(slot + 1, 1)
             if closed is not None and slot >= NORMALISE_BEHIND:
                 normalise(slot - NORMALISE_BEHIND)
-            if slot == SLOTS:
-                normalise(LAST)
             if slot < LAST:
                 shift_max(slot + 1)
             for s in range(SLOTS):
@@ -425,12 +442,27 @@ def tile_mhla2_pa_t_kernel(tc, x_k, W_K, v_heads, out):
                 quantise_v(v_slots.index(slot))
             if phase in (1, 2) and q < QUADS - 1:
                 quantise_x((q + 1) * GROUP_SLOTS + phase - 1)
-            if QUANTISE_P_BEHIND <= slot < SLOTS:
+            if slot >= QUANTISE_P_BEHIND:
                 quantise_p(slot - QUANTISE_P_BEHIND)
-            if slot == SLOTS:
-                quantise_p(LAST - 1)
-                quantise_p(LAST)
-            for s in range(SLOTS):
-                summary_slot = min(s + QUANTISE_P_BEHIND + 4, SLOTS)
-                if summary_slot == slot and (s // QUAD_SLOTS) % QUADS_PER_BATCH == QUADS_PER_BATCH - 1:
-                    summarise(s)
+            if slot == LAST:
+                normalise(slot - NORMALISE_BEHIND)
+                for h in range(H - HALF_HEADS, H):
+                    if h < H - PIECE_HEADS:
+                        open_summary(h, k_psum, "k_bank")
+                    else:
+                        open_summary(h, t_psum, "turned")
+                summarise(LAST - 3, o_psum, "summary")
+            done = slot - QUANTISE_P_BEHIND - 4
+            if 0 <= done < SLOTS // B and done // QUAD_SLOTS == QUADS_PER_BATCH - 1:
+                summarise(done, o_psum, "summary")
+
+        invert(GROUPS - 1)
+        quantise_p(LAST - 2)
+        spread_inverse(GROUPS - 1)
+        summarise(LAST - 2, k_psum, "k_bank")
+        normalise(LAST - 1)
+        normalise(LAST)
+        quantise_p(LAST - 1)
+        quantise_p(LAST)
+        close_summaries(QUAD_SLOTS - 2)
+        close_summaries(QUAD_SLOTS - 1)

@@ -240,12 +240,13 @@ def tile_mhla2_pa_t_kernel(tc, x_k, W_K, v_heads, out):
                     op=MULT,
                 )
 
-            if s in (SLOTS - 3, SLOTS - 2):
+            if s in (1, SLOTS - 3, SLOTS - 2):
                 multiply(nc.vector, inv_banks[group], 0, 0, DH)
                 multiply(nc.vector, inv_banks[group], 1, 0, DH)
             else:
                 multiply(nc.gpsimd, inv_sums[group], 1, 0, DH)
-                multiply(nc.vector, inv_banks[group], 0, 0, DH)
+                multiply(nc.vector, inv_banks[group], 0, 0, DH - 24)
+                multiply(nc.gpsimd, inv_sums[group], 0, DH - 24, DH)
 
         def quantise_p(s):
             q, piece = s // QUAD_SLOTS, s % QUAD_SLOTS
@@ -271,7 +272,7 @@ def tile_mhla2_pa_t_kernel(tc, x_k, W_K, v_heads, out):
             for i in range(PIECE_HEADS):
                 h = piece * PIECE_HEADS + i
                 g = h % HALF_HEADS
-                split = DH if i == 0 or s >= 28 else 32
+                split = DH if i == 0 or s >= 28 else 24
                 if split > 0:
                     regroup_head(nc.scalar.copy, v_raw[q], v_grouped[group], h, g, 0, split)
                 if split < DH:
@@ -328,8 +329,8 @@ def tile_mhla2_pa_t_kernel(tc, x_k, W_K, v_heads, out):
                 copy(out=result[:, i], in_=last_banks[h][:])
             store(B - 1, piece, result)
 
-        load_x(0, 0, 2)
         load_w(0, 0)
+        load_x(0, 0, 2)
         load_w(0, 1)
         load_x(0, 2, 4)
         load_w(1, 0)
@@ -350,19 +351,17 @@ def tile_mhla2_pa_t_kernel(tc, x_k, W_K, v_heads, out):
         w_scales = keep.tile([P, FEATURE_PASSES, H * DH], U8, name="w_scales", align_bytes=64)
 
         ctx.enter_context(tc.manual_schedule())
-        V_HEADS, S_HEADS = (0, 1, 2), (3,)
+        def regroup_w_shared(n, g, vector_heads):
+            regroup_w(n, g, range(vector_heads), nc.vector.tensor_copy)
+            regroup_w(n, g, range(vector_heads, HALF_HEADS), nc.scalar.copy)
 
-        def regroup_w_shared(n, g):
-            regroup_w(n, g, V_HEADS, nc.vector.tensor_copy)
-            regroup_w(n, g, S_HEADS, nc.scalar.copy)
-
+        regroup_w_shared(0, 0, 3)
+        quantise_w(0, 0)
         transpose_x(0)
         transpose_x(1)
         copy_x(0)
-        regroup_w_shared(0, 0)
-        quantise_w(0, 0)
         copy_x(1)
-        regroup_w_shared(0, 1)
+        regroup_w_shared(0, 1, 2)
         quantise_x(0)
         quantise_w(0, 1)
         transpose_x(2)
@@ -371,12 +370,12 @@ def tile_mhla2_pa_t_kernel(tc, x_k, W_K, v_heads, out):
         copy_x(3)
         for i in range(SLOT_TILES):
             project(0, i)
-        regroup_w(1, 0, (0, 1, 2), nc.vector.tensor_copy)
+        regroup_w(1, 0, range(2), nc.vector.tensor_copy)
         quantise_x(1)
         for i in range(SLOT_TILES):
             row_max(0, i)
-        regroup_w(1, 0, (3,), nc.scalar.copy)
-        regroup_w(1, 1, (0, 1), nc.scalar.copy)
+        regroup_w(1, 0, range(2, HALF_HEADS), nc.scalar.copy)
+        regroup_w(1, 1, range(2), nc.scalar.copy)
         shift_max(0)
         for i in range(SLOT_TILES):
             project(1, i)
@@ -434,7 +433,7 @@ def tile_mhla2_pa_t_kernel(tc, x_k, W_K, v_heads, out):
                 if regroup_v_slot(s) == slot:
                     regroup_v(s)
             if slot == 0:
-                regroup_w(1, 1, (2, 3), nc.vector.tensor_copy)
+                regroup_w(1, 1, range(2, HALF_HEADS), nc.vector.tensor_copy)
                 for g in range(FEATURE_PASSES):
                     quantise_w(1, g)
 

@@ -51,13 +51,11 @@ def tile_mhla2_pa_t_kernel(tc, x_k, W_K, v_heads, out):
         keep = ctx.enter_context(tc.tile_pool(name="keep", bufs=1))
         x_rows = ctx.enter_context(tc.tile_pool(name="x_rows", bufs=4))
         v_rows = ctx.enter_context(tc.tile_pool(name="v_rows", bufs=4))
-        w_rows = ctx.enter_context(tc.tile_pool(name="w_rows", bufs=4))
-        w_grouped_pool = ctx.enter_context(tc.tile_pool(name="w_grouped", bufs=2))
         v_grouped_pool = ctx.enter_context(tc.tile_pool(name="v_grouped", bufs=4))
         grouped_pool = ctx.enter_context(tc.tile_pool(name="grouped", bufs=2))
         x_grouped_pool = ctx.enter_context(tc.tile_pool(name="x_grouped", bufs=3))
         x_mx = ctx.enter_context(tc.tile_pool(name="x_mx", bufs=6))
-        quad_mx = ctx.enter_context(tc.tile_pool(name="quad_mx", bufs=QUADS_PER_BATCH + 2))
+        quad_mx = ctx.enter_context(tc.tile_pool(name="quad_mx", bufs=QUADS))
         exp_pool = ctx.enter_context(tc.tile_pool(name="exp", bufs=3))
         stats = ctx.enter_context(tc.tile_pool(name="stats", bufs=4))
         result_pool = ctx.enter_context(tc.tile_pool(name="result", bufs=4))
@@ -69,7 +67,7 @@ def tile_mhla2_pa_t_kernel(tc, x_k, W_K, v_heads, out):
         x_raw, turned_x, v_raw, v_grouped, v_codes, v_scales = {}, {}, {}, {}, {}, {}
         x_grouped, x_codes, x_scales, k_banks, largest, shift = {}, {}, {}, {}, {}, {}
         exps, sums, inv_sums, inv_banks, p_grouped, p_codes, p_scales = {}, {}, {}, {}, {}, {}, {}
-        w_grouped, last_banks = {}, {}
+        w_grouped, last_banks, v_banks = {}, {}, {}
 
         def quad_rows(q):
             first = (q % QUADS_PER_BATCH) * K_PASS
@@ -101,17 +99,18 @@ def tile_mhla2_pa_t_kernel(tc, x_k, W_K, v_heads, out):
 
         def load_w(n, g):
             heads = slice(n * HALF_HEADS, (n + 1) * HALF_HEADS)
-            w_raw[n, g] = w_rows.tile([P, HALF_HEADS, PACK, DH], BF16, name="w_raw", tag="w_raw")
+            if g == 0:
+                w_raw[n] = v_rows.tile([P, FEATURE_PASSES, HALF_HEADS, PACK, DH], BF16, name="w_raw", tag="v_raw")
             rows = W_K[heads, g * K_PASS : (g + 1) * K_PASS, :]
-            nc.sync.dma_start(out=w_raw[n, g][:], in_=rows.rearrange("h (p t) c -> p h t c", t=PACK))
+            nc.sync.dma_start(out=w_raw[n][:, g], in_=rows.rearrange("h (p t) c -> p h t c", t=PACK))
 
         def regroup_w(n, g, heads, copy):
             if heads[0] == 0:
-                w_grouped[n, g] = w_grouped_pool.tile(
-                    [P, HALF_HEADS, DH, PACK], BF16, name="w_grouped", tag="w_grouped", align_bytes=64
+                w_grouped[n, g] = v_grouped_pool.tile(
+                    [P, HALF_HEADS, DH, PACK], BF16, name="w_grouped", tag="v_grouped", align_bytes=64
                 )
             for h in heads:
-                regroup_head(copy, w_raw[n, g], w_grouped[n, g], h, h)
+                regroup_head(copy, w_raw[n][:, g], w_grouped[n, g], h, h)
 
         def quantise_w(n, g):
             cols = slice(n * BANK, (n + 1) * BANK)
@@ -263,16 +262,41 @@ def tile_mhla2_pa_t_kernel(tc, x_k, W_K, v_heads, out):
                     out=v_raw[q][:, heads], in_=v_heads[b, heads, rows, :].rearrange("h (p t) c -> p h t c", t=PACK)
                 )
 
-        def regroup_v(s):
-            q, piece, group = s // QUAD_SLOTS, s % QUAD_SLOTS, s // GROUP_SLOTS
+        def by_product(s):
+            return s not in (SLOTS - QUAD_SLOTS, SLOTS - 2)
+
+        def interleave_v(s):
+            q, piece = s // QUAD_SLOTS, s % QUAD_SLOTS
+            v_banks[s] = o_psum.tile([P, 1, DH * PACK], BF16, name="v_bank", tag="summary")
+            for i in range(1):
+                nc.tensor.matmul(
+                    out=v_banks[s][:, i],
+                    lhsT=identity_bf16[:],
+                    rhs=v_raw[q][:, piece * PIECE_HEADS + i].rearrange("p t c -> p c t"),
+                    start=True,
+                    stop=True,
+                )
+
+        def new_v_grouped(s):
             if s % GROUP_SLOTS == 0:
-                v_grouped[group] = v_grouped_pool.tile(
+                v_grouped[s // GROUP_SLOTS] = v_grouped_pool.tile(
                     [P, HALF_HEADS, DH, PACK], BF16, name="v_grouped", tag="v_grouped", align_bytes=64
                 )
-            for i in range(PIECE_HEADS):
+
+        def fetch_v(s):
+            g = (s % GROUP_SLOTS) * PIECE_HEADS
+            nc.scalar.copy(
+                out=v_grouped[s // GROUP_SLOTS][:, g : g + 1].rearrange("p h c t -> p (h c t)"),
+                in_=v_banks[s][:].rearrange("p h c -> p (h c)"),
+            )
+
+        def regroup_v(s):
+            q, piece, group = s // QUAD_SLOTS, s % QUAD_SLOTS, s // GROUP_SLOTS
+            new_v_grouped(s)
+            for i in range(1 if by_product(s) else 0, PIECE_HEADS):
                 h = piece * PIECE_HEADS + i
                 g = h % HALF_HEADS
-                split = DH if i == 0 or s >= 28 else 24
+                split = DH if i == 0 or s >= 99 else 64
                 if split > 0:
                     regroup_head(nc.scalar.copy, v_raw[q], v_grouped[group], h, g, 0, split)
                 if split < DH:
@@ -342,6 +366,8 @@ def tile_mhla2_pa_t_kernel(tc, x_k, W_K, v_heads, out):
 
         identity = keep.tile([P, P], F32, name="identity")
         make_identity(nc, identity[:])
+        identity_bf16 = keep.tile([P, P], BF16, name="identity_bf16")
+        make_identity(nc, identity_bf16[:])
         zero = keep.tile([P, 1], F32, name="zero")
         one = keep.tile([P, 1], F32, name="one")
         nc.vector.memset(zero[:], 0.0)
@@ -388,7 +414,7 @@ def tile_mhla2_pa_t_kernel(tc, x_k, W_K, v_heads, out):
             return max(t - X_AHEAD, -1)
 
         def regroup_v_slot(s):
-            return s + 1 - s // 8
+            return s + 1 if s < SLOTS - QUAD_SLOTS else SLOTS - QUAD_SLOTS + (s - SLOTS + QUAD_SLOTS + 1) // 2
 
         v_slots = [s for s in range(SLOTS) if s % QUAD_SLOTS in (0, 3) or s >= SLOTS - QUAD_SLOTS]
         v_slots = v_slots[-GROUPS:]
@@ -406,6 +432,9 @@ def tile_mhla2_pa_t_kernel(tc, x_k, W_K, v_heads, out):
 
             if 0 < slot < LAST:
                 project(slot + 1, 0)
+            for s in range(SLOTS):
+                if regroup_v_slot(s) == slot - 1 and by_product(s):
+                    fetch_v(s)
             exponentials(slot, 0)
             for t in range(PACK, TILES):
                 if turn_slot(t) == slot - 1:
@@ -417,6 +446,9 @@ def tile_mhla2_pa_t_kernel(tc, x_k, W_K, v_heads, out):
                 project(slot + 1, 1)
             if closed is not None:
                 spread_inverse(closed)
+            for s in range(SLOTS):
+                if regroup_v_slot(s) == slot and by_product(s):
+                    interleave_v(s)
             exponentials(slot, 1)
 
             if slot < LAST:
@@ -451,9 +483,9 @@ def tile_mhla2_pa_t_kernel(tc, x_k, W_K, v_heads, out):
                     else:
                         open_summary(h, t_psum, "turned")
                 summarise(LAST - 3, o_psum, "summary")
-            done = slot - QUANTISE_P_BEHIND - 4
-            if 0 <= done < SLOTS // B and done // QUAD_SLOTS == QUADS_PER_BATCH - 1:
-                summarise(done, o_psum, "summary")
+            done = slot - (TILES - X_AHEAD)
+            if 0 <= done < QUAD_SLOTS:
+                summarise(SLOTS // B - QUAD_SLOTS + done, t_psum, "turned")
 
         invert(GROUPS - 1)
         quantise_p(LAST - 2)

@@ -39,6 +39,8 @@ SOFTMAX_SCALE = 1.0 / DH**0.25
 X_AHEAD = 6
 NORMALISE_BEHIND = GROUP_SLOTS
 QUANTISE_P_BEHIND = NORMALISE_BEHIND + 1
+PRODUCT_COLS = 96
+SCALAR_COLS = 64
 X_LOAD_AHEAD = 3
 V_LOAD_AHEAD = 2
 
@@ -263,42 +265,38 @@ def tile_mhla2_pa_t_kernel(tc, x_k, W_K, v_heads, out):
                 )
 
         def by_product(s):
-            return s not in (SLOTS - QUAD_SLOTS, SLOTS - 2)
+            return s != SLOTS - 2
 
         def interleave_v(s):
             q, piece = s // QUAD_SLOTS, s % QUAD_SLOTS
-            v_banks[s] = o_psum.tile([P, 1, DH * PACK], BF16, name="v_bank", tag="summary")
-            for i in range(1):
-                nc.tensor.matmul(
-                    out=v_banks[s][:, i],
-                    lhsT=identity_bf16[:],
-                    rhs=v_raw[q][:, piece * PIECE_HEADS + i].rearrange("p t c -> p c t"),
-                    start=True,
-                    stop=True,
-                )
-
-        def new_v_grouped(s):
-            if s % GROUP_SLOTS == 0:
-                v_grouped[s // GROUP_SLOTS] = v_grouped_pool.tile(
-                    [P, HALF_HEADS, DH, PACK], BF16, name="v_grouped", tag="v_grouped", align_bytes=64
-                )
+            v_banks[s] = o_psum.tile([P, PRODUCT_COLS * PACK], BF16, name="v_bank", tag="summary")
+            nc.tensor.matmul(
+                out=v_banks[s][:],
+                lhsT=identity_bf16[:],
+                rhs=v_raw[q][:, piece * PIECE_HEADS, :, 0:PRODUCT_COLS].rearrange("p t c -> p c t"),
+                start=True,
+                stop=True,
+            )
 
         def fetch_v(s):
             g = (s % GROUP_SLOTS) * PIECE_HEADS
             nc.scalar.copy(
-                out=v_grouped[s // GROUP_SLOTS][:, g : g + 1].rearrange("p h c t -> p (h c t)"),
-                in_=v_banks[s][:].rearrange("p h c -> p (h c)"),
+                out=v_grouped[s // GROUP_SLOTS][:, g, 0:PRODUCT_COLS].rearrange("p c t -> p (c t)"), in_=v_banks[s][:]
             )
 
         def regroup_v(s):
             q, piece, group = s // QUAD_SLOTS, s % QUAD_SLOTS, s // GROUP_SLOTS
-            new_v_grouped(s)
-            for i in range(1 if by_product(s) else 0, PIECE_HEADS):
+            if s % GROUP_SLOTS == 0:
+                v_grouped[group] = v_grouped_pool.tile(
+                    [P, HALF_HEADS, DH, PACK], BF16, name="v_grouped", tag="v_grouped", align_bytes=64
+                )
+            for i in range(PIECE_HEADS):
                 h = piece * PIECE_HEADS + i
                 g = h % HALF_HEADS
-                split = DH if i == 0 or s >= 99 else 64
-                if split > 0:
-                    regroup_head(nc.scalar.copy, v_raw[q], v_grouped[group], h, g, 0, split)
+                first = PRODUCT_COLS if i == 0 and by_product(s) else 0
+                split = DH if i == 0 else SCALAR_COLS
+                if first < split:
+                    regroup_head(nc.scalar.copy, v_raw[q], v_grouped[group], h, g, first, split)
                 if split < DH:
                     regroup_head(nc.vector.tensor_copy, v_raw[q], v_grouped[group], h, g, split, DH)
 
@@ -414,7 +412,7 @@ def tile_mhla2_pa_t_kernel(tc, x_k, W_K, v_heads, out):
             return max(t - X_AHEAD, -1)
 
         def regroup_v_slot(s):
-            return s + 1 if s < SLOTS - QUAD_SLOTS else SLOTS - QUAD_SLOTS + (s - SLOTS + QUAD_SLOTS + 1) // 2
+            return s if s < SLOTS - 2 else s - 1
 
         v_slots = [s for s in range(SLOTS) if s % QUAD_SLOTS in (0, 3) or s >= SLOTS - QUAD_SLOTS]
         v_slots = v_slots[-GROUPS:]

@@ -241,13 +241,16 @@ def tile_mhla2_pa_t_kernel(tc, x_k, W_K, v_heads, out):
                     op=MULT,
                 )
 
-            if s in (1, SLOTS - 3, SLOTS - 2):
+            if s in (1, SLOTS - 2):
                 multiply(nc.vector, inv_banks[group], 0, 0, DH)
                 multiply(nc.vector, inv_banks[group], 1, 0, DH)
+            elif s == SLOTS - 3:
+                multiply(nc.gpsimd, inv_sums[group], 1, 0, DH)
+                multiply(nc.vector, inv_banks[group], 0, 0, DH)
             else:
                 multiply(nc.gpsimd, inv_sums[group], 1, 0, DH)
-                multiply(nc.vector, inv_banks[group], 0, 0, DH - 24)
-                multiply(nc.gpsimd, inv_sums[group], 0, DH - 24, DH)
+                multiply(nc.vector, inv_banks[group], 0, 0, DH - 20)
+                multiply(nc.gpsimd, inv_sums[group], 0, DH - 20, DH)
 
         def quantise_p(s):
             q, piece = s // QUAD_SLOTS, s % QUAD_SLOTS
@@ -437,13 +440,13 @@ def tile_mhla2_pa_t_kernel(tc, x_k, W_K, v_heads, out):
             for t in range(PACK, TILES):
                 if turn_slot(t) == slot - 1:
                     copy_x(t)
-            for t in range(PACK, TILES):
-                if turn_slot(t) == slot:
-                    transpose_x(t)
             if 0 < slot < LAST:
                 project(slot + 1, 1)
             if closed is not None:
                 spread_inverse(closed)
+            for t in range(PACK, TILES):
+                if turn_slot(t) == slot:
+                    transpose_x(t)
             for s in range(SLOTS):
                 if regroup_v_slot(s) == slot and by_product(s):
                     interleave_v(s)
@@ -451,7 +454,7 @@ def tile_mhla2_pa_t_kernel(tc, x_k, W_K, v_heads, out):
 
             if slot < LAST:
                 row_max(slot + 1, 0)
-            if closed is None and NORMALISE_BEHIND <= slot < LAST:
+            if closed is None and slot >= NORMALISE_BEHIND:
                 normalise(slot - NORMALISE_BEHIND)
             if slot < LAST:
                 row_max(slot + 1, 1)
@@ -471,23 +474,23 @@ def tile_mhla2_pa_t_kernel(tc, x_k, W_K, v_heads, out):
                 quantise_v(v_slots.index(slot))
             if phase in (1, 2) and q < QUADS - 1:
                 quantise_x((q + 1) * GROUP_SLOTS + phase - 1)
-            if slot >= QUANTISE_P_BEHIND:
+            if QUANTISE_P_BEHIND <= slot < LAST:
                 quantise_p(slot - QUANTISE_P_BEHIND)
             if slot == LAST:
-                normalise(slot - NORMALISE_BEHIND)
                 for h in range(H - HALF_HEADS, H):
                     if h < H - PIECE_HEADS:
                         open_summary(h, k_psum, "k_bank")
                     else:
                         open_summary(h, t_psum, "turned")
-                summarise(LAST - 3, o_psum, "summary")
             done = slot - (TILES - X_AHEAD)
             if 0 <= done < QUAD_SLOTS:
                 summarise(SLOTS // B - QUAD_SLOTS + done, t_psum, "turned")
 
         invert(GROUPS - 1)
-        quantise_p(LAST - 2)
         spread_inverse(GROUPS - 1)
+        quantise_p(LAST - 3)
+        summarise(LAST - 3, o_psum, "summary")
+        quantise_p(LAST - 2)
         summarise(LAST - 2, k_psum, "k_bank")
         normalise(LAST - 1)
         normalise(LAST)

@@ -39,8 +39,8 @@ SOFTMAX_SCALE = 1.0 / DH**0.25
 X_AHEAD = 6
 NORMALISE_BEHIND = GROUP_SLOTS
 QUANTISE_P_BEHIND = NORMALISE_BEHIND + 1
-PRODUCT_COLS = 96
-SCALAR_COLS = 64
+PRODUCT_COLS = 128
+SCALAR_COLS = 72
 X_LOAD_AHEAD = 3
 V_LOAD_AHEAD = 2
 
@@ -268,15 +268,15 @@ def tile_mhla2_pa_t_kernel(tc, x_k, W_K, v_heads, out):
                 )
 
         def by_product(s):
-            return s != SLOTS - 2
+            return s != SLOTS - 1
 
         def interleave_v(s):
             q, piece = s // QUAD_SLOTS, s % QUAD_SLOTS
             v_banks[s] = o_psum.tile([P, PRODUCT_COLS * PACK], BF16, name="v_bank", tag="summary")
             nc.tensor.matmul(
-                out=v_banks[s][:],
+                out=v_banks[s][:].rearrange("p (c i t) -> p c t i", i=4, t=PACK),
                 lhsT=identity_bf16[:],
-                rhs=v_raw[q][:, piece * PIECE_HEADS, :, 0:PRODUCT_COLS].rearrange("p t c -> p c t"),
+                rhs=v_raw[q][:, piece * PIECE_HEADS, :, 0:PRODUCT_COLS].rearrange("p t (c i) -> p c t i", i=4),
                 start=True,
                 stop=True,
             )
@@ -415,7 +415,7 @@ def tile_mhla2_pa_t_kernel(tc, x_k, W_K, v_heads, out):
             return max(t - X_AHEAD, -1)
 
         def regroup_v_slot(s):
-            return s if s < SLOTS - 2 else s - 1
+            return min(s, SLOTS - 2)
 
         v_slots = [s for s in range(SLOTS) if s % QUAD_SLOTS in (0, 3) or s >= SLOTS - QUAD_SLOTS]
         v_slots = v_slots[-GROUPS:]
@@ -462,13 +462,13 @@ def tile_mhla2_pa_t_kernel(tc, x_k, W_K, v_heads, out):
                 normalise(slot - NORMALISE_BEHIND)
             if slot < LAST:
                 shift_max(slot + 1)
-            for s in range(SLOTS):
-                if regroup_v_slot(s) == slot:
-                    regroup_v(s)
             if slot == 0:
                 regroup_w(1, 1, range(2, HALF_HEADS), nc.vector.tensor_copy)
                 for g in range(FEATURE_PASSES):
                     quantise_w(1, g)
+            for s in range(SLOTS):
+                if regroup_v_slot(s) == slot:
+                    regroup_v(s)
 
             if slot in v_slots:
                 quantise_v(v_slots.index(slot))

from contextlib import ExitStack

import concourse.mybir as mybir
from concourse.masks import make_identity

F32 = mybir.dt.float32
BF16 = mybir.dt.bfloat16
U32 = mybir.dt.uint32
U8 = mybir.dt.uint8
FP8X4 = mybir.dt.float8_e4m3fn_x4
EXP = mybir.ActivationFunctionType.Exp
MAX = mybir.AluOpType.max
MULT = mybir.AluOpType.mult
ADD = mybir.AluOpType.add
AXIS_X = mybir.AxisListType.X

B, S, D, H, DH = 2, 2048, 1024, 8, 128
P = 128
PACK = 4
K_PASS = P * PACK
BANK = 512

FEATURE_PASSES = D // K_PASS
QUADS_PER_BATCH = S // K_PASS
QUADS = B * QUADS_PER_BATCH
TILES = QUADS * PACK
HALVES = H * DH // BANK
HALF_HEADS = H // HALVES
SLOT_TILES = 2
GROUP_SLOTS = PACK // SLOT_TILES
GROUPS = QUADS * HALVES
SLOTS = GROUPS * GROUP_SLOTS
QUAD_SLOTS = HALVES * GROUP_SLOTS
PIECE_HEADS = H // QUAD_SLOTS
PIECE_COLS = PIECE_HEADS * DH

SOFTMAX_SCALE = 1.0 / DH**0.25

X_AHEAD = 6
NORMALISE_BEHIND = GROUP_SLOTS
QUANTISE_P_BEHIND = NORMALISE_BEHIND + 1
PRODUCT_COLS = 128
SCALAR_COLS = 72
X_LOAD_AHEAD = 3
V_LOAD_AHEAD = 2

FLOPS = 2 * B * S * D * H * DH + 2 * B * H * S * DH * DH


def tile_mhla2_pa_t_kernel(tc, x_k, W_K, v_heads, out):
    nc = tc.nc
    with ExitStack() as ctx:
        keep = ctx.enter_context(tc.tile_pool(name="keep", bufs=1))
        x_rows = ctx.enter_context(tc.tile_pool(name="x_rows", bufs=4))
        v_rows = ctx.enter_context(tc.tile_pool(name="v_rows", bufs=4))
        v_grouped_pool = ctx.enter_context(tc.tile_pool(name="v_grouped", bufs=4))
        grouped_pool = ctx.enter_context(tc.tile_pool(name="grouped", bufs=2))
        x_grouped_pool = ctx.enter_context(tc.tile_pool(name="x_grouped", bufs=3))
        x_mx = ctx.enter_context(tc.tile_pool(name="x_mx", bufs=6))
        quad_mx = ctx.enter_context(tc.tile_pool(name="quad_mx", bufs=QUADS))
        exp_pool = ctx.enter_context(tc.tile_pool(name="exp", bufs=3))
        stats = ctx.enter_context(tc.tile_pool(name="stats", bufs=4))
        result_pool = ctx.enter_context(tc.tile_pool(name="result", bufs=4))
        k_psum = ctx.enter_context(tc.psum_pool(name="k_psum", bufs=4))
        o_psum = ctx.enter_context(tc.psum_pool(name="o_psum", bufs=1))
        t_psum = ctx.enter_context(tc.psum_pool(name="t_psum", bufs=2))
        i_psum = ctx.enter_context(tc.psum_pool(name="i_psum", bufs=1))

        x_raw, turned_x, v_raw, v_grouped, v_codes, v_scales = {}, {}, {}, {}, {}, {}
        x_grouped, x_codes, x_scales, k_banks, largest, shift = {}, {}, {}, {}, {}, {}
        exps, sums, inv_sums, inv_banks, p_grouped, p_codes, p_scales = {}, {}, {}, {}, {}, {}, {}
        w_grouped, last_banks, v_banks = {}, {}, {}

        def quad_rows(q):
            first = (q % QUADS_PER_BATCH) * K_PASS
            return q // QUADS_PER_BATCH, slice(first, first + K_PASS)

        def regroup_head(copy, raw, grouped, h, g, first=0, last=DH):
            copy(
                out=grouped[:, g, first:last].rearrange("p (c i) t -> p c t i", i=4),
                in_=raw[:, h, :, first:last].rearrange("p t (c i) -> p c t i", i=4),
            )

        def gpsimd_copy(out, in_):
            nc.gpsimd.tensor_scalar(out=out, in0=in_, scalar1=1.0, scalar2=0.0, op0=MULT, op1=ADD)

        def new_quad_mx(name):
            codes = quad_mx.tile([P, H * DH], U32, name=name + "_codes", tag=name + "_codes", align_bytes=64)
            scales = quad_mx.tile([P, H * DH], U8, name=name + "_scales", tag=name + "_scales", align_bytes=64)
            return codes, scales

        def quantise_piece(grouped, codes, scales, piece):
            cols = slice(piece * PIECE_COLS, (piece + 1) * PIECE_COLS)
            nc.vector.quantize_mx(
                out=codes[:, cols].bitcast(FP8X4),
                scales=scales[:, cols],
                in_=grouped[:].rearrange("p h c t -> p (h c t)"),
            )

        w_raw = {}

        def load_w(n, g):
            heads = slice(n * HALF_HEADS, (n + 1) * HALF_HEADS)
            if g == 0:
                w_raw[n] = v_rows.tile([P, FEATURE_PASSES, HALF_HEADS, PACK, DH], BF16, name="w_raw", tag="v_raw")
            rows = W_K[heads, g * K_PASS : (g + 1) * K_PASS, :]
            nc.sync.dma_start(out=w_raw[n][:, g], in_=rows.rearrange("h (p t) c -> p h t c", t=PACK))

        def regroup_w(n, g, heads, copy):
            if heads[0] == 0:
                w_grouped[n, g] = v_grouped_pool.tile(
                    [P, HALF_HEADS, DH, PACK], BF16, name="w_grouped", tag="v_grouped", align_bytes=64
                )
            for h in heads:
                regroup_head(copy, w_raw[n][:, g], w_grouped[n, g], h, h)

        def quantise_w(n, g):
            cols = slice(n * BANK, (n + 1) * BANK)
            nc.vector.quantize_mx(
                out=w_codes[:, g, cols].bitcast(FP8X4),
                scales=w_scales[:, g, cols],
                in_=w_grouped[n, g][:].rearrange("p h c t -> p (h c t)"),
            )

        def load_x(q, first, last, tiles=1):
            b, rows = quad_rows(q)
            if first == 0:
                x_raw[q] = x_rows.tile([P, PACK, D], BF16, name="x_raw", tag="x_raw")
            source = x_k[b, rows, :].rearrange("(p j) d -> p j d", j=PACK)
            for j in range(first, last, tiles):
                nc.sync.dma_start(out=x_raw[q][:, j : j + tiles], in_=source[:, j : j + tiles])

        def transpose_x(t):
            words = x_raw[t // PACK][:, t % PACK, :].bitcast(F32)
            pass_words = K_PASS // 2
            turned = t_psum.tile([P, FEATURE_PASSES, 2, P], F32, name="turned", tag="turned")
            for g in range(FEATURE_PASSES):
                for u in range(2):
                    nc.tensor.transpose(
                        turned[:, g, u, :],
                        words[:, g * pass_words + u : (g + 1) * pass_words : 2],
                        identity[:],
                    )
            turned_x[t] = turned

        def copy_x(t):
            pair, i = t // SLOT_TILES, t % SLOT_TILES
            if i == 0:
                x_grouped[pair] = x_grouped_pool.tile(
                    [P, SLOT_TILES * D], BF16, name="x_grouped", tag="x_grouped", align_bytes=64
                )
            nc.scalar.copy(
                out=x_grouped[pair][:, i * D : (i + 1) * D].bitcast(F32).rearrange("p (g r u) -> p g r u", g=FEATURE_PASSES, u=2),
                in_=turned_x[t][:].rearrange("p g u r -> p g r u"),
            )

        def quantise_x(pair):
            x_codes[pair] = x_mx.tile([P, SLOT_TILES * D // PACK], U32, name="x_codes", tag="x_codes", align_bytes=64)
            x_scales[pair] = x_mx.tile([P, SLOT_TILES * D // PACK], U8, name="x_scales", tag="x_scales", align_bytes=64)
            nc.vector.quantize_mx(
                out=x_codes[pair][:].bitcast(FP8X4), scales=x_scales[pair][:], in_=x_grouped[pair][:]
            )

        def slot_pair(s):
            return (s // QUAD_SLOTS) * GROUP_SLOTS + s % GROUP_SLOTS

        def project(s, i):
            n = (s // GROUP_SLOTS) % HALVES
            cols = slice(n * BANK, (n + 1) * BANK)
            pair = slot_pair(s)
            bank = k_psum.tile([P, BANK], F32, name="k_bank", tag="k_bank")
            for g in range(FEATURE_PASSES):
                first = (i * FEATURE_PASSES + g) * P
                tokens = slice(first, first + P)
                nc.tensor.matmul_mx(
                    out=bank[:],
                    lhsT=x_codes[pair][:, tokens].bitcast(FP8X4),
                    lhsT_scale=x_scales[pair][:, tokens],
                    rhs=w_codes[:, g, cols].bitcast(FP8X4),
                    rhs_scale=w_scales[:, g, cols],
                    start=(g == 0),
                    stop=(g == FEATURE_PASSES - 1),
                )
            k_banks[s, i] = bank

        def row_max(s, i):
            if i == 0:
                largest[s] = stats.tile([P, SLOT_TILES * HALF_HEADS], F32, name="largest", tag="largest")
            nc.vector.tensor_reduce(
                out=largest[s][:, i * HALF_HEADS : (i + 1) * HALF_HEADS],
                in_=k_banks[s, i][:].rearrange("p (h c) -> p h c", h=HALF_HEADS),
                axis=AXIS_X,
                op=MAX,
            )

        def shift_max(s):
            shift[s] = stats.tile([P, SLOT_TILES * HALF_HEADS], F32, name="shift", tag="shift")
            nc.scalar.mul(out=shift[s][:], in_=largest[s][:], mul=-SOFTMAX_SCALE)

        def exponentials(s, i):
            group = s // GROUP_SLOTS
            j = (s % GROUP_SLOTS) * SLOT_TILES + i
            if j == 0:
                exps[group] = exp_pool.tile([P, PACK, BANK], F32, name="exps", tag="exps")
                sums[group] = stats.tile([P, HALF_HEADS * PACK], F32, name="sums", tag="sums")
            for h in range(HALF_HEADS):
                nc.scalar.activation(
                    out=exps[group][:, j, h * DH : (h + 1) * DH],
                    in_=k_banks[s, i][:, h * DH : (h + 1) * DH],
                    func=EXP,
                    bias=shift[s][:, i * HALF_HEADS + h : i * HALF_HEADS + h + 1],
                    scale=SOFTMAX_SCALE,
                    accum_out=sums[group][:, h * PACK + j : h * PACK + j + 1],
                )

        def invert(group):
            inv_sums[group] = stats.tile([P, HALF_HEADS * PACK], F32, name="inv_sums", tag="inv_sums")
            nc.vector.reciprocal(out=inv_sums[group][:], in_=sums[group][:])

        def spread_inverse(group):
            inv_banks[group] = i_psum.tile([P, HALF_HEADS * PACK], F32, name="inv_bank", tag="inv_bank")
            nc.tensor.matmul(
                out=inv_banks[group][:], lhsT=identity[:], rhs=inv_sums[group][:], start=True, stop=True
            )

        def normalise(s):
            group, piece = s // GROUP_SLOTS, s % GROUP_SLOTS
            p_grouped[s] = grouped_pool.tile(
                [P, PIECE_HEADS, DH, PACK], BF16, name="p_grouped", tag="p_grouped", align_bytes=64
            )

            def multiply(engine, inverse, i, first, last):
                h = piece * PIECE_HEADS + i
                engine.tensor_tensor(
                    out=p_grouped[s][:, i, first:last].rearrange("p (c i) j -> p c j i", i=4),
                    in0=exps[group][:, :, h * DH + first : h * DH + last].rearrange("p j (c i) -> p c j i", i=4),
                    in1=inverse[:, h * PACK : (h + 1) * PACK]
                    .unsqueeze(1)
                    .unsqueeze(3)
                    .to_broadcast([P, (last - first) // 4, PACK, 4]),
                    op=MULT,
                )

            if s in (1, SLOTS - 2):
                multiply(nc.vector, inv_banks[group], 0, 0, DH)
                multiply(nc.vector, inv_banks[group], 1, 0, DH)
            elif s == SLOTS - 3:
                multiply(nc.gpsimd, inv_sums[group], 1, 0, DH)
                multiply(nc.vector, inv_banks[group], 0, 0, DH)
            else:
                multiply(nc.gpsimd, inv_sums[group], 1, 0, DH)
                multiply(nc.vector, inv_banks[group], 0, 0, DH - 20)
                multiply(nc.gpsimd, inv_sums[group], 0, DH - 20, DH)

        def quantise_p(s):
            q, piece = s // QUAD_SLOTS, s % QUAD_SLOTS
            if piece == 0:
                p_codes[q], p_scales[q] = new_quad_mx("p")
            quantise_piece(p_grouped[s], p_codes[q], p_scales[q], piece)

        def load_v(q):
            b, rows = quad_rows(q)
            v_raw[q] = v_rows.tile([P, H, PACK, DH], BF16, name="v_raw", tag="v_raw")
            for piece in range(QUAD_SLOTS):
                heads = slice(piece * PIECE_HEADS, (piece + 1) * PIECE_HEADS)
                nc.sync.dma_start(
                    out=v_raw[q][:, heads], in_=v_heads[b, heads, rows, :].rearrange("h (p t) c -> p h t c", t=PACK)
                )

        def by_product(s):
            return s != SLOTS - 1

        def interleave_v(s):
            q, piece = s // QUAD_SLOTS, s % QUAD_SLOTS
            v_banks[s] = o_psum.tile([P, PRODUCT_COLS * PACK], BF16, name="v_bank", tag="summary")
            nc.tensor.matmul(
                out=v_banks[s][:].rearrange("p (c i t) -> p c t i", i=4, t=PACK),
                lhsT=identity_bf16[:],
                rhs=v_raw[q][:, piece * PIECE_HEADS, :, 0:PRODUCT_COLS].rearrange("p t (c i) -> p c t i", i=4),
                start=True,
                stop=True,
            )

        def fetch_v(s):
            g = (s % GROUP_SLOTS) * PIECE_HEADS
            nc.scalar.copy(
                out=v_grouped[s // GROUP_SLOTS][:, g, 0:PRODUCT_COLS].rearrange("p c t -> p (c t)"), in_=v_banks[s][:]
            )

        def regroup_v(s):
            q, piece, group = s // QUAD_SLOTS, s % QUAD_SLOTS, s // GROUP_SLOTS
            if s % GROUP_SLOTS == 0:
                v_grouped[group] = v_grouped_pool.tile(
                    [P, HALF_HEADS, DH, PACK], BF16, name="v_grouped", tag="v_grouped", align_bytes=64
                )
            for i in range(PIECE_HEADS):
                h = piece * PIECE_HEADS + i
                g = h % HALF_HEADS
                first = PRODUCT_COLS if i == 0 and by_product(s) else 0
                split = DH if i == 0 else SCALAR_COLS
                if first < split:
                    regroup_head(nc.scalar.copy, v_raw[q], v_grouped[group], h, g, first, split)
                if split < DH:
                    regroup_head(nc.vector.tensor_copy, v_raw[q], v_grouped[group], h, g, split, DH)

        def quantise_v(group):
            q, n = group // HALVES, group % HALVES
            if n == 0:
                v_codes[q], v_scales[q] = new_quad_mx("v")
            cols = slice(n * BANK, (n + 1) * BANK)
            nc.vector.quantize_mx(
                out=v_codes[q][:, cols].bitcast(FP8X4),
                scales=v_scales[q][:, cols],
                in_=v_grouped[group][:].rearrange("p h c t -> p (h c t)"),
            )

        def add_quads(b, h, quads, bank):
            cols = slice(h * DH, (h + 1) * DH)
            for n in quads:
                q = b * QUADS_PER_BATCH + n
                nc.tensor.matmul_mx(
                    out=bank,
                    lhsT=p_codes[q][:, cols].bitcast(FP8X4),
                    lhsT_scale=p_scales[q][:, cols],
                    rhs=v_codes[q][:, cols].bitcast(FP8X4),
                    rhs_scale=v_scales[q][:, cols],
                    start=(n == 0),
                    stop=(n == QUADS_PER_BATCH - 1),
                )

        def store(b, piece, result):
            heads = slice(piece * PIECE_HEADS, (piece + 1) * PIECE_HEADS)
            nc.sync.dma_start(out=out[b, heads].rearrange("h c e -> c h e"), in_=result[:])

        def summarise(s, pool, tag):
            b, piece = s // QUAD_SLOTS // QUADS_PER_BATCH, s % QUAD_SLOTS
            summary = pool.tile([P, PIECE_HEADS, DH], F32, name="summary", tag=tag)
            for i in range(PIECE_HEADS):
                add_quads(b, piece * PIECE_HEADS + i, range(QUADS_PER_BATCH), summary[:, i])
            result = result_pool.tile([P, PIECE_HEADS, DH], F32, name="result", tag="result")
            nc.scalar.copy(out=result[:], in_=summary[:])
            store(b, piece, result)

        def open_summary(h, pool, tag):
            last_banks[h] = pool.tile([P, DH], F32, name="last_bank", tag=tag)
            add_quads(B - 1, h, range(QUADS_PER_BATCH - 1), last_banks[h][:])

        def close_summaries(piece):
            result = result_pool.tile([P, PIECE_HEADS, DH], F32, name="result", tag="result")
            for i in range(PIECE_HEADS):
                h = piece * PIECE_HEADS + i
                add_quads(B - 1, h, (QUADS_PER_BATCH - 1,), last_banks[h][:])
                copy = nc.scalar.copy if i == 0 else nc.vector.tensor_copy
                copy(out=result[:, i], in_=last_banks[h][:])
            store(B - 1, piece, result)

        load_w(0, 0)
        load_x(0, 0, 2)
        load_w(0, 1)
        load_x(0, 2, 4)
        load_w(1, 0)
        load_w(1, 1)
        load_x(1, 0, 4)
        load_v(0)
        load_x(2, 0, 4, PACK)
        load_v(1)

        identity = keep.tile([P, P], F32, name="identity")
        make_identity(nc, identity[:])
        identity_bf16 = keep.tile([P, P], BF16, name="identity_bf16")
        make_identity(nc, identity_bf16[:])
        zero = keep.tile([P, 1], F32, name="zero")
        one = keep.tile([P, 1], F32, name="one")
        nc.vector.memset(zero[:], 0.0)
        nc.scalar.activation(out=one[:], in_=zero[:], func=EXP)

        w_codes = keep.tile([P, FEATURE_PASSES, H * DH], U32, name="w_codes", align_bytes=64)
        w_scales = keep.tile([P, FEATURE_PASSES, H * DH], U8, name="w_scales", align_bytes=64)

        ctx.enter_context(tc.manual_schedule())
        def regroup_w_shared(n, g, vector_heads):
            regroup_w(n, g, range(vector_heads), nc.vector.tensor_copy)
            regroup_w(n, g, range(vector_heads, HALF_HEADS), nc.scalar.copy)

        regroup_w_shared(0, 0, 3)
        quantise_w(0, 0)
        transpose_x(0)
        transpose_x(1)
        copy_x(0)
        copy_x(1)
        regroup_w_shared(0, 1, 2)
        quantise_x(0)
        quantise_w(0, 1)
        transpose_x(2)
        transpose_x(3)
        copy_x(2)
        copy_x(3)
        for i in range(SLOT_TILES):
            project(0, i)
        regroup_w(1, 0, range(2), nc.vector.tensor_copy)
        quantise_x(1)
        for i in range(SLOT_TILES):
            row_max(0, i)
        regroup_w(1, 0, range(2, HALF_HEADS), nc.scalar.copy)
        regroup_w(1, 1, range(2), nc.scalar.copy)
        shift_max(0)
        for i in range(SLOT_TILES):
            project(1, i)
        transpose_x(4)
        transpose_x(5)

        LAST = SLOTS - 1

        def turn_slot(t):
            return max(t - X_AHEAD, -1)

        def regroup_v_slot(s):
            return min(s, SLOTS - 2)

        v_slots = [s for s in range(SLOTS) if s % QUAD_SLOTS in (0, 3) or s >= SLOTS - QUAD_SLOTS]
        v_slots = v_slots[-GROUPS:]

        for slot in range(SLOTS):
            q, phase = slot // QUAD_SLOTS, slot % QUAD_SLOTS
            if phase == 0 and q + X_LOAD_AHEAD < QUADS:
                load_x(q + X_LOAD_AHEAD, 0, 4, PACK)
            if phase == 0 and q + V_LOAD_AHEAD < QUADS:
                load_v(q + V_LOAD_AHEAD)

            closed = (slot - 1) // GROUP_SLOTS if slot > 0 and phase % GROUP_SLOTS == 0 else None
            if closed is not None:
                invert(closed)

            if 0 < slot < LAST:
                project(slot + 1, 0)
            for s in range(SLOTS):
                if regroup_v_slot(s) == slot - 1 and by_product(s):
                    fetch_v(s)
            exponentials(slot, 0)
            for t in range(PACK, TILES):
                if turn_slot(t) == slot - 1:
                    copy_x(t)
            if 0 < slot < LAST:
                project(slot + 1, 1)
            if closed is not None:
                spread_inverse(closed)
            for t in range(PACK, TILES):
                if turn_slot(t) == slot:
                    transpose_x(t)
            for s in range(SLOTS):
                if regroup_v_slot(s) == slot and by_product(s):
                    interleave_v(s)
            exponentials(slot, 1)

            if slot < LAST:
                row_max(slot + 1, 0)
            if closed is None and slot >= NORMALISE_BEHIND:
                normalise(slot - NORMALISE_BEHIND)
            if slot < LAST:
                row_max(slot + 1, 1)
            if closed is not None and slot >= NORMALISE_BEHIND:
                normalise(slot - NORMALISE_BEHIND)
            if slot < LAST:
                shift_max(slot + 1)
            if slot == 0:
                regroup_w(1, 1, range(2, HALF_HEADS), nc.vector.tensor_copy)
                for g in range(FEATURE_PASSES):
                    quantise_w(1, g)
            for s in range(SLOTS):
                if regroup_v_slot(s) == slot:
                    regroup_v(s)

            if slot in v_slots:
                quantise_v(v_slots.index(slot))
            if phase in (1, 2) and q < QUADS - 1:
                quantise_x((q + 1) * GROUP_SLOTS + phase - 1)
            if QUANTISE_P_BEHIND <= slot < LAST:
                quantise_p(slot - QUANTISE_P_BEHIND)
            if slot == LAST:
                for h in range(H - HALF_HEADS, H):
                    if h < H - PIECE_HEADS:
                        open_summary(h, k_psum, "k_bank")
                    else:
                        open_summary(h, t_psum, "turned")
            done = slot - (TILES - X_AHEAD)
            if 0 <= done < QUAD_SLOTS:
                summarise(SLOTS // B - QUAD_SLOTS + done, t_psum, "turned")

        invert(GROUPS - 1)
        spread_inverse(GROUPS - 1)
        quantise_p(LAST - 3)
        summarise(LAST - 3, o_psum, "summary")
        quantise_p(LAST - 2)
        summarise(LAST - 2, k_psum, "k_bank")
        normalise(LAST - 1)
        normalise(LAST)
        quantise_p(LAST - 1)
        quantise_p(LAST)
        close_summaries(QUAD_SLOTS - 2)
        close_summaries(QUAD_SLOTS - 1)
